import numpy as np
import ml_dtypes


def mxq(x, axis, fmt="e4m3"):
    dtype, down = {"e4m3": (ml_dtypes.float8_e4m3fn, 7), "e5m2": (ml_dtypes.float8_e5m2, 14)}[fmt]
    v = np.moveaxis(np.asarray(x, np.float32).astype(ml_dtypes.bfloat16).astype(np.float64), axis, -1)
    blocks = v.reshape(v.shape[:-1] + (-1, 32))
    amax = np.abs(blocks).max(-1, keepdims=True)
    byte = np.maximum(np.where(amax > 0, np.frexp(amax)[1] - 1 + 127, 0) - down, 1)
    scale = np.exp2(byte - 127.0)
    codes = (blocks / scale).astype(np.float32).astype(dtype).astype(np.float64)
    return np.moveaxis((codes * scale).reshape(v.shape), -1, axis)


WIDE = False


def mx_kscale(k):
    if not WIDE:
        return np.ones(k)
    levels = np.array([10, -10, 5, -5, 0])
    if k % 512:
        return np.exp2(np.random.permutation(np.resize(levels, k // 32))).repeat(32)
    a = np.empty((k // 512, 16))
    for p in range(k // 512):
        a[p, :8] = np.random.permutation(np.resize(levels, 8))
        for g in range(8):
            far = levels[np.abs(levels - a[p, g]) >= 10]
            a[p, g + 8] = far[np.random.randint(len(far))]
    return np.exp2(a.ravel()).repeat(32)


BF16 = ml_dtypes.bfloat16


def bf(x):
    return np.asarray(x, np.float32).astype(BF16)


def f64(x):
    return np.asarray(x).astype(np.float64)


B, T, D, NH, NG = 4, 512, 1024, 8, 4
GH = (D // NH) * NG
JIT = 0.06


def angles(t, d):
    i = np.arange(d // 2, dtype=np.float64)
    theta = (10000.0 ** (-(2.0 * (i - 1.0)))) / d
    return np.arange(t, dtype=np.float64)[:, None] * theta[None, :]


def rope(y, cos, sin):
    ye, yo = y[..., 0::2], y[..., 1::2]
    oe = ye * cos + yo * sin
    oo = -ye * sin + yo * cos
    return np.stack([oe, oo], axis=-1).reshape(y.shape)


def draw0():
    s = mx_kscale(D)
    aq = angles(T, D) + JIT * np.random.standard_normal((T, D // 2))
    ak = angles(T, GH) + JIT * np.random.standard_normal((T, GH // 2))
    return {"x": bf(np.random.standard_normal((B, T, D)) * s),
            "Wq": bf(np.random.standard_normal((D, D)) / np.sqrt(D) / s[:, None]),
            "Wk": bf(np.random.standard_normal((D, GH)) / np.sqrt(D) / s[:, None]),
            "Wv": bf(np.random.standard_normal((D, GH)) / np.sqrt(D) / s[:, None]),
            "cos_q": bf(np.cos(aq)), "sin_q": bf(np.sin(aq)),
            "cos_k": bf(np.cos(ak)), "sin_k": bf(np.sin(ak))}


def core(x, Wq, Wk, Wv, cos_q, sin_q, cos_k, sin_k):
    xq = mxq(f64(x), 2, "e4m3")
    q = rope(xq @ mxq(f64(Wq), 0, "e4m3"), f64(cos_q), f64(sin_q))
    k = rope(xq @ mxq(f64(Wk), 0, "e4m3"), f64(cos_k), f64(sin_k))
    v = xq @ mxq(f64(Wv), 0, "e4m3")
    return q, k, v


def e4m3fn_bytes(y):
    return np.clip(np.asarray(y, np.float64), -448.0, 448.0).astype(np.float32).astype(ml_dtypes.float8_e4m3fn).view(np.uint8)


def e4m3fn_values(b):
    return np.asarray(b, np.uint8).view(ml_dtypes.float8_e4m3fn).astype(np.float64)


def setup_inputs():
    d = draw0()
    x0 = np.asarray(d['x']).astype(np.float64)
    s = (np.max(np.abs(x0), axis=(0, 1), keepdims=True) / 448.0).astype(np.float32)
    out = {}
    for k, v in d.items():
        if k == 'x':
            out['x_bytes'] = e4m3fn_bytes(x0 / s.astype(np.float64))
            out['x_scale'] = s
        else:
            out[k] = v
    return out


def reference(x_bytes, x_scale, Wq, Wk, Wv, cos_q, sin_q, cos_k, sin_k):
    return core(e4m3fn_values(x_bytes) * x_scale.astype(np.float64), Wq, Wk, Wv, cos_q, sin_q, cos_k, sin_k)

@@ -1,0 +1,332 @@
+from contextlib import ExitStack
+
+import concourse.mybir as mybir
+from concourse.masks import make_identity
+
+F32 = mybir.dt.float32
+BF16 = mybir.dt.bfloat16
+U8 = mybir.dt.uint8
+U32 = mybir.dt.uint32
+FP8 = mybir.dt.float8_e4m3fn
+FP8X4 = mybir.dt.float8_e4m3fn_x4
+MULT = mybir.AluOpType.mult
+ADD = mybir.AluOpType.add
+
+P = 128
+TOKENS = 2048
+K = 1024
+PASSES = 2
+NT = TOKENS // P
+NB = 512
+PAIRS = NB // 2
+FLOPS = 2 * TOKENS * K * 2048
+
+VSH = 384
+SC_TILES = (6, 8, 9, 10, 12, 13, 14, 15)
+VADD = ((3, 2), (6, 2), (9, 2), (12, 2), (15, 1), (15, 2))
+COPY = mybir.ActivationFunctionType.Copy
+
+
+def tile_selfattn_pa_kernel(
+    tc, x_bytes, x_scale, Wq, Wk, Wv, cos_q, sin_q, cos_k, sin_k, out_0, out_1, out_2
+):
+    nc = tc.nc
+    xf = x_bytes.flatten_outer_dims()
+    oq = out_0.flatten_outer_dims()
+    ok = out_1.flatten_outer_dims()
+    ov = out_2.flatten_outer_dims()
+    w_src = [Wq[:, 0:NB], Wq[:, NB : 2 * NB], Wk, Wv]
+    o_dst = [oq[:, 0:NB], oq[:, NB : 2 * NB], ok, ov]
+
+    with ExitStack() as ctx:
+        keep = ctx.enter_context(tc.tile_pool(name="keep", bufs=1))
+        xbfp = ctx.enter_context(tc.tile_pool(name="xbfp", bufs=3))
+        xgp = ctx.enter_context(tc.tile_pool(name="xgp", bufs=3))
+        xpp = ctx.enter_context(tc.tile_pool(name="xpp", bufs=2))
+        wgp = ctx.enter_context(tc.tile_pool(name="wgp", bufs=2))
+        rp = ctx.enter_context(tc.tile_pool(name="rp", bufs=6))
+        vp = ctx.enter_context(tc.tile_pool(name="vp", bufs=4))
+        pst = ctx.enter_context(tc.psum_pool(name="pst", bufs=2))
+        psa = ctx.enter_context(tc.psum_pool(name="psa", bufs=6))
+
+        ident = keep.tile([P, P], F32, name="ident")
+        make_identity(nc, ident[:])
+
+        sk = keep.tile([P, PASSES, 4], F32, name="sk")
+        nc.sync.dma_start(
+            out=sk[:], in_=x_scale.rearrange("a b k -> (a b k)").rearrange("(g p t) -> p g t", p=P, t=4)
+        )
+        xb = []
+        wraw = []
+        tq = []
+        tk = []
+        for j in range(NT // 2):
+            xb.append(keep.tile([P, 2, K], U8, name="xb%d" % j))
+        for nb in range(4):
+            wraw.append(keep.tile([P, PASSES, 4, NB], BF16, name="wraw%d" % nb))
+        for tt in range(4):
+            tq.append(keep.tile([P, 3, 2 * PAIRS], BF16, name="tq%d" % tt))
+            tk.append(keep.tile([P, 3, PAIRS], BF16, name="tk%d" % tt))
+
+        def load_x(j):
+            nc.sync.dma_start(
+                out=xb[j][:],
+                in_=xf[2 * j * P : (2 * j + 2) * P, :].rearrange("(n p) k -> p n k", p=P),
+            )
+
+        def load_w(nb):
+            for g in range(PASSES):
+                nc.sync.dma_start(
+                    out=wraw[nb][:, g],
+                    in_=w_src[nb][g * 512 : (g + 1) * 512, :].rearrange("(p j) n -> p j n", j=4),
+                )
+
+        def load_tq(tt):
+            nc.sync.dma_start(out=tq[tt][:, 0, :], in_=sin_q[tt * P : (tt + 1) * P, :])
+            nc.sync.dma_start(out=tq[tt][:, 1, :], in_=cos_q[tt * P : (tt + 1) * P, :])
+
+        def load_tk(tt):
+            nc.sync.dma_start(out=tk[tt][:, 0, :], in_=sin_k[tt * P : (tt + 1) * P, :])
+            nc.sync.dma_start(out=tk[tt][:, 1, :], in_=cos_k[tt * P : (tt + 1) * P, :])
+
+        load_x(0)
+        load_w(0)
+        load_tq(0)
+        load_tq(1)
+        load_x(1)
+        load_w(1)
+        load_tq(2)
+        load_tq(3)
+        load_x(2)
+        load_w(2)
+        load_x(3)
+        for tt in range(4):
+            load_tk(tt)
+        load_w(3)
+        for j in range(4, NT // 2):
+            load_x(j)
+
+        def negate(t, eng):
+            eng.tensor_scalar(
+                out=t[:, 2, :], in0=t[:, 0, :], scalar1=-1.0, scalar2=0.0, op0=MULT, op1=ADD
+            )
+
+        xbf = {}
+        xt = {}
+        xg = {}
+        xc = {}
+        xs = {}
+
+        def cast(i):
+            if i >= NT:
+                return
+            xbf[i] = xbfp.tile([P, K], BF16, name="xbf")
+            nc.scalar.copy(out=xbf[i][:], in_=xb[i // 2][:, i % 2, :].bitcast(FP8))
+
+        def turn(i):
+            if i >= NT:
+                return
+            xt[i] = pst.tile([P, PASSES, 2, P], F32, name="xt")
+            words = xbf[i][:].bitcast(F32)
+            for g in range(PASSES):
+                for u in range(2):
+                    nc.tensor.transpose(
+                        xt[i][:, g, u, :], words[:, 256 * g + u : 256 * (g + 1) : 2], ident[:]
+                    )
+
+        def scale(i):
+            if i >= NT:
+                return
+            xg[i] = xgp.tile([P, PASSES, P, 4], BF16, name="xg", align_bytes=64)
+            for g in range(PASSES):
+                nc.vector.tensor_tensor(
+                    out=xg[i][:, g].rearrange("p r (u e) -> p r u e", u=2),
+                    in0=xt[i][:, g].bitcast(BF16).rearrange("p u (r e) -> p r u e", e=2),
+                    in1=sk[:, g, :]
+                    .rearrange("p (u e) -> p u e", u=2)
+                    .unsqueeze(1)
+                    .to_broadcast([P, P, 2, 2]),
+                    op=MULT,
+                )
+
+        def scale_on_scalar(i):
+            xpl = xpp.tile([P, PASSES, 4, P], BF16, name="xpl")
+            for g in range(PASSES):
+                for u in range(2):
+                    halves = xt[i][:, g, u, :].bitcast(BF16).rearrange("p (r e) -> p r e", e=2)
+                    for e in range(2):
+                        t = 2 * u + e
+                        nc.scalar.activation(
+                            out=xpl[:, g, t, :],
+                            in_=halves[:, :, e],
+                            func=COPY,
+                            scale=sk[:, g, t : t + 1],
+                        )
+            xg[i] = xgp.tile([P, PASSES, P, 4], BF16, name="xg", align_bytes=64)
+            nc.scalar.copy(out=xg[i][:], in_=xpl[:].rearrange("p g t r -> p g r t"))
+
+        def quant(i):
+            if i >= NT:
+                return
+            xc[i] = keep.tile([P, PASSES * P], U32, name="xc%d" % i, align_bytes=64)
+            xs[i] = keep.tile([P, PASSES * P], U8, name="xs%d" % i, align_bytes=64)
+            nc.vector.quantize_mx(
+                out=xc[i][:].bitcast(FP8X4),
+                scales=xs[i][:],
+                in_=xg[i][:].rearrange("p g r t -> p (g r t)"),
+            )
+
+        wg = {}
+        wc = []
+        ws = []
+        for nb in range(4):
+            wc.append(keep.tile([P, PASSES, NB], U32, name="wc%d" % nb, align_bytes=64))
+            ws.append(keep.tile([P, PASSES, NB], U8, name="ws%d" % nb, align_bytes=64))
+
+        def wcopy(nb, g, c0, c1, on_vector):
+            if nb not in wg:
+                wg[nb] = wgp.tile([P, PASSES, NB, 4], BF16, name="wg", align_bytes=64)
+            dst = wg[nb][:, g, c0:c1, :]
+            src = wraw[nb][:, g, :, c0:c1].rearrange("p j n -> p n j")
+            if on_vector:
+                nc.vector.tensor_copy(out=dst, in_=src)
+            else:
+                nc.scalar.copy(out=dst, in_=src)
+
+        def wquant(nb, g):
+            nc.vector.quantize_mx(
+                out=wc[nb][:, g, :].bitcast(FP8X4),
+                scales=ws[nb][:, g, :],
+                in_=wg[nb][:, g].rearrange("p n j -> p (n j)"),
+            )
+
+        acc = {}
+        xy = {}
+
+        def mm(un):
+            i, nb = un
+            acc[un] = psa.tile([P, NB], F32, name="acc")
+            for g in range(PASSES):
+                nc.tensor.matmul_mx(
+                    out=acc[un][:],
+                    lhsT=xc[i][:, g * P : (g + 1) * P].bitcast(FP8X4),
+                    lhsT_scale=xs[i][:, g * P : (g + 1) * P],
+                    rhs=wc[nb][:, g, :].bitcast(FP8X4),
+                    rhs_scale=ws[nb][:, g, :],
+                    start=(g == 0),
+                    stop=(g == PASSES - 1),
+                )
+
+        def table(un):
+            i, nb = un
+            if nb == 2:
+                return tk[i % 4][:, :, :]
+            return tq[i % 4][:, :, nb * PAIRS : (nb + 1) * PAIRS]
+
+        def rope_half(un, e):
+            t = table(un)
+            if e == 0:
+                xy[un] = rp.tile([P, 2, PAIRS, 2], F32, name="rxy")
+            nc.vector.tensor_tensor(
+                out=xy[un][:, e],
+                in0=acc[un][:]
+                .rearrange("p (i e) -> p i e", e=2)[:, :, e : e + 1]
+                .to_broadcast([P, PAIRS, 2]),
+                in1=t[:, 1 - e : 3 - e, :].rearrange("p h i -> p i h"),
+                op=MULT,
+            )
+
+        def store(un, src):
+            i, nb = un
+            nc.sync.dma_start(out=o_dst[nb][i * P : (i + 1) * P, :], in_=src)
+
+        def finish(un):
+            a = xy[un][:, 0]
+            b = xy[un][:, 1]
+            eng = nc.gpsimd
+            if un in VADD:
+                eng = nc.vector
+            eng.tensor_tensor(out=a, in0=a, in1=b, op=ADD)
+            store(un, a.rearrange("p i e -> p (i e)"))
+
+        def vcopy(un):
+            o = vp.tile([P, NB], F32, name="vo")
+            nc.scalar.copy(out=o[:], in_=acc[un][:])
+            store(un, o[:])
+
+        deferred = []
+
+        def flush():
+            for fn, arg in deferred:
+                fn(arg)
+            deferred.clear()
+
+        def xprep(i):
+            if i >= NT:
+                return
+            cast(i)
+            turn(i)
+            if i in SC_TILES:
+                scale_on_scalar(i)
+            else:
+                scale(i)
+            deferred.append((quant, i))
+
+        def unit(un):
+            mm(un)
+            if un[1] == 3:
+                vcopy(un)
+                return
+            rope_half(un, 0)
+            rope_half(un, 1)
+            flush()
+            if un in VADD:
+                deferred.append((finish, un))
+            else:
+                finish(un)
+
+        cast(0)
+        cast(1)
+        turn(0)
+        wcopy(0, 0, 0, VSH, True)
+        wcopy(0, 0, VSH, NB, False)
+        scale(0)
+        wcopy(0, 1, 0, VSH, True)
+        wcopy(0, 1, VSH, NB, False)
+        wquant(0, 0)
+        quant(0)
+        wquant(0, 1)
+        cast(2)
+        turn(1)
+        for tt in range(4):
+            negate(tq[tt], nc.gpsimd)
+        scale(1)
+        quant(1)
+        turn(2)
+        scale(2)
+        quant(2)
+
+        later = [(1, 0), (1, 1), (2, 0), (2, 1), (3, 0), (3, 1)]
+        ready = [0]
+        done = set()
+        for i in range(NT):
+            if i < len(later):
+                nb, g = later[i]
+                wcopy(nb, g, 0, NB // 2, False)
+                wcopy(nb, g, NB // 2, NB, False)
+                wquant(nb, g)
+                if g == PASSES - 1:
+                    ready.append(nb)
+            if i == 2:
+                for tt in range(4):
+                    negate(tk[tt], nc.vector)
+            xprep(i + 3)
+            order = [0, 1, 2, 3]
+            if i == NT - 1:
+                order = [3, 0, 1, 2]
+            for j in range(i + 1):
+                for nb in order:
+                    if nb in ready and (j, nb) not in done:
+                        done.add((j, nb))
+                        unit((j, nb))
+        flush()

@@ -65,8 +65,8 @@ def tile_selfattn_pa_kernel(
         for nb in range(4):
             wraw.append(keep.tile([P, PASSES, 4, NB], BF16, name="wraw%d" % nb))
         for tt in range(4):
-            tq.append(keep.tile([P, 3, 2 * PAIRS], BF16, name="tq%d" % tt))
-            tk.append(keep.tile([P, 3, PAIRS], BF16, name="tk%d" % tt))
+            tq.append(keep.tile([P, 4, 2 * PAIRS], BF16, name="tq%d" % tt))
+            tk.append(keep.tile([P, 4, PAIRS], BF16, name="tk%d" % tt))
 
         def load_x(j):
             nc.sync.dma_start(
@@ -82,12 +82,14 @@ def tile_selfattn_pa_kernel(
                 )
 
         def load_tq(tt):
-            nc.sync.dma_start(out=tq[tt][:, 0, :], in_=sin_q[tt * P : (tt + 1) * P, :])
-            nc.sync.dma_start(out=tq[tt][:, 1, :], in_=cos_q[tt * P : (tt + 1) * P, :])
+            nc.sync.dma_start(out=tq[tt][:, 2, :], in_=sin_q[tt * P : (tt + 1) * P, :])
+            nc.sync.dma_start(out=tq[tt][:, 0, :], in_=cos_q[tt * P : (tt + 1) * P, :])
+            nc.sync.dma_start(out=tq[tt][:, 3, :], in_=cos_q[tt * P : (tt + 1) * P, :])
 
         def load_tk(tt):
-            nc.sync.dma_start(out=tk[tt][:, 0, :], in_=sin_k[tt * P : (tt + 1) * P, :])
-            nc.sync.dma_start(out=tk[tt][:, 1, :], in_=cos_k[tt * P : (tt + 1) * P, :])
+            nc.sync.dma_start(out=tk[tt][:, 2, :], in_=sin_k[tt * P : (tt + 1) * P, :])
+            nc.sync.dma_start(out=tk[tt][:, 0, :], in_=cos_k[tt * P : (tt + 1) * P, :])
+            nc.sync.dma_start(out=tk[tt][:, 3, :], in_=cos_k[tt * P : (tt + 1) * P, :])
 
         load_x(0)
         load_w(0)
@@ -108,7 +110,7 @@ def tile_selfattn_pa_kernel(
 
         def negate(t, eng):
             eng.tensor_scalar(
-                out=t[:, 2, :], in0=t[:, 0, :], scalar1=-1.0, scalar2=0.0, op0=MULT, op1=ADD
+                out=t[:, 1, :], in0=t[:, 2, :], scalar1=-1.0, scalar2=0.0, op0=MULT, op1=ADD
             )
 
         xbf = {}
@@ -223,16 +225,15 @@ def tile_selfattn_pa_kernel(
                 return tk[i % 4][:, :, :]
             return tq[i % 4][:, :, nb * PAIRS : (nb + 1) * PAIRS]
 
-        def rope_half(un, e):
-            t = table(un)
-            if e == 0:
-                xy[un] = rp.tile([P, 2, PAIRS, 2], F32, name="rxy")
+        def rope_products(un):
+            xy[un] = rp.tile([P, 2, PAIRS, 2], F32, name="rxy")
             nc.vector.tensor_tensor(
-                out=xy[un][:, e],
+                out=xy[un][:],
                 in0=acc[un][:]
-                .rearrange("p (i e) -> p i e", e=2)[:, :, e : e + 1]
-                .to_broadcast([P, PAIRS, 2]),
-                in1=t[:, 1 - e : 3 - e, :].rearrange("p h i -> p i h"),
+                .rearrange("p (i e) -> p e i", e=2)
+                .unsqueeze(3)
+                .to_broadcast([P, 2, PAIRS, 2]),
+                in1=table(un).rearrange("p (e h) i -> p e i h", e=2),
                 op=MULT,
             )
 
@@ -277,8 +278,7 @@ def tile_selfattn_pa_kernel(
             if un[1] == 3:
                 vcopy(un)
                 return
-            rope_half(un, 0)
-            rope_half(un, 1)
+            rope_products(un)
             flush()
             if un in VADD:
                 deferred.append((finish, un))

@@ -84,12 +84,10 @@ def tile_selfattn_pa_kernel(
         def load_tq(tt):
             nc.sync.dma_start(out=tq[tt][:, 2, :], in_=sin_q[tt * P : (tt + 1) * P, :])
             nc.sync.dma_start(out=tq[tt][:, 0, :], in_=cos_q[tt * P : (tt + 1) * P, :])
-            nc.sync.dma_start(out=tq[tt][:, 3, :], in_=cos_q[tt * P : (tt + 1) * P, :])
 
         def load_tk(tt):
             nc.sync.dma_start(out=tk[tt][:, 2, :], in_=sin_k[tt * P : (tt + 1) * P, :])
             nc.sync.dma_start(out=tk[tt][:, 0, :], in_=cos_k[tt * P : (tt + 1) * P, :])
-            nc.sync.dma_start(out=tk[tt][:, 3, :], in_=cos_k[tt * P : (tt + 1) * P, :])
 
         load_x(0)
         load_w(0)
@@ -111,6 +109,9 @@ def tile_selfattn_pa_kernel(
         def negate(t, eng):
             eng.tensor_scalar(
                 out=t[:, 1, :], in0=t[:, 2, :], scalar1=-1.0, scalar2=0.0, op0=MULT, op1=ADD
+            )
+            eng.tensor_scalar(
+                out=t[:, 3, :], in0=t[:, 0, :], scalar1=1.0, scalar2=0.0, op0=MULT, op1=ADD
             )
 
         xbf = {}

@@ -22,7 +22,7 @@ PAIRS = NB // 2
 FLOPS = 2 * TOKENS * K * 2048
 
 VSH = 384
-SC_TILES = (6, 8, 9, 10, 12, 13, 14, 15)
+SC_PAIRS = (4, 5, 6, 7)
 VADD = ((3, 2), (6, 2), (9, 2), (12, 2), (15, 1), (15, 2))
 COPY = mybir.ActivationFunctionType.Copy
 
@@ -40,8 +40,8 @@ def tile_selfattn_pa_kernel(
 
     with ExitStack() as ctx:
         keep = ctx.enter_context(tc.tile_pool(name="keep", bufs=1))
-        xbfp = ctx.enter_context(tc.tile_pool(name="xbfp", bufs=3))
-        xgp = ctx.enter_context(tc.tile_pool(name="xgp", bufs=3))
+        xbfp = ctx.enter_context(tc.tile_pool(name="xbfp", bufs=2))
+        xgp = ctx.enter_context(tc.tile_pool(name="xgp", bufs=2))
         xpp = ctx.enter_context(tc.tile_pool(name="xpp", bufs=2))
         wgp = ctx.enter_context(tc.tile_pool(name="wgp", bufs=2))
         rp = ctx.enter_context(tc.tile_pool(name="rp", bufs=6))
@@ -119,64 +119,64 @@ def tile_selfattn_pa_kernel(
         xg = {}
         xc = {}
         xs = {}
+        xpl = {}
 
         def cast(i):
-            if i >= NT:
-                return
-            xbf[i] = xbfp.tile([P, K], BF16, name="xbf")
-            nc.scalar.copy(out=xbf[i][:], in_=xb[i // 2][:, i % 2, :].bitcast(FP8))
+            j, n = divmod(i, 2)
+            if n == 0:
+                xbf[j] = xbfp.tile([P, 2, K], BF16, name="xbf")
+            nc.scalar.copy(out=xbf[j][:, n, :], in_=xb[j][:, n, :].bitcast(FP8))
 
-        def turn(i):
-            if i >= NT:
-                return
-            xt[i] = pst.tile([P, PASSES, 2, P], F32, name="xt")
-            words = xbf[i][:].bitcast(F32)
+        def turn(j):
             for g in range(PASSES):
-                for u in range(2):
-                    nc.tensor.transpose(
-                        xt[i][:, g, u, :], words[:, 256 * g + u : 256 * (g + 1) : 2], ident[:]
-                    )
-
-        def scale(i):
-            if i >= NT:
-                return
-            xg[i] = xgp.tile([P, PASSES, P, 4], BF16, name="xg", align_bytes=64)
-            for g in range(PASSES):
-                nc.vector.tensor_tensor(
-                    out=xg[i][:, g].rearrange("p r (u e) -> p r u e", u=2),
-                    in0=xt[i][:, g].bitcast(BF16).rearrange("p u (r e) -> p r u e", e=2),
-                    in1=sk[:, g, :]
-                    .rearrange("p (u e) -> p u e", u=2)
-                    .unsqueeze(1)
-                    .to_broadcast([P, P, 2, 2]),
-                    op=MULT,
-                )
-
-        def scale_on_scalar(i):
-            xpl = xpp.tile([P, PASSES, 4, P], BF16, name="xpl")
-            for g in range(PASSES):
-                for u in range(2):
-                    halves = xt[i][:, g, u, :].bitcast(BF16).rearrange("p (r e) -> p r e", e=2)
-                    for e in range(2):
-                        t = 2 * u + e
-                        nc.scalar.activation(
-                            out=xpl[:, g, t, :],
-                            in_=halves[:, :, e],
-                            func=COPY,
-                            scale=sk[:, g, t : t + 1],
+                xt[(j, g)] = pst.tile([P, 2, 2, P], F32, name="xt")
+                for n in range(2):
+                    words = xbf[j][:, n, :].bitcast(F32)
+                    for u in range(2):
+                        nc.tensor.transpose(
+                            xt[(j, g)][:, u, n, :], words[:, 256 * g + u : 256 * (g + 1) : 2], ident[:]
                         )
-            xg[i] = xgp.tile([P, PASSES, P, 4], BF16, name="xg", align_bytes=64)
-            nc.scalar.copy(out=xg[i][:], in_=xpl[:].rearrange("p g t r -> p g r t"))
 
-        def quant(i):
-            if i >= NT:
-                return
-            xc[i] = keep.tile([P, PASSES * P], U32, name="xc%d" % i, align_bytes=64)
-            xs[i] = keep.tile([P, PASSES * P], U8, name="xs%d" % i, align_bytes=64)
+        def halfwords(j, g):
+            return xt[(j, g)][:].rearrange("p u n r -> p u (n r)").bitcast(BF16)
+
+        def scale(j, g):
+            if g == 0:
+                xg[j] = xgp.tile([P, PASSES, 2 * P, 4], BF16, name="xg", align_bytes=64)
+            nc.vector.tensor_tensor(
+                out=xg[j][:, g].rearrange("p m (u e) -> p m u e", u=2),
+                in0=halfwords(j, g).rearrange("p u (m e) -> p m u e", e=2),
+                in1=sk[:, g, :]
+                .rearrange("p (u e) -> p u e", u=2)
+                .unsqueeze(1)
+                .to_broadcast([P, 2 * P, 2, 2]),
+                op=MULT,
+            )
+
+        def scale_on_scalar(j, g):
+            if g == 0:
+                xpl[j] = xpp.tile([P, PASSES, 4, 2 * P], BF16, name="xpl")
+            for u in range(2):
+                halves = halfwords(j, g)[:, u, :].rearrange("p (m e) -> p m e", e=2)
+                for e in range(2):
+                    t = 2 * u + e
+                    nc.scalar.activation(
+                        out=xpl[j][:, g, t, :],
+                        in_=halves[:, :, e],
+                        func=COPY,
+                        scale=sk[:, g, t : t + 1],
+                    )
+            if g == PASSES - 1:
+                xg[j] = xgp.tile([P, PASSES, 2 * P, 4], BF16, name="xg", align_bytes=64)
+                nc.scalar.copy(out=xg[j][:], in_=xpl[j][:].rearrange("p g t m -> p g m t"))
+
+        def quant(j):
+            xc[j] = keep.tile([P, PASSES, 2 * P], U32, name="xc%d" % j, align_bytes=64)
+            xs[j] = keep.tile([P, PASSES, 2 * P], U8, name="xs%d" % j, align_bytes=64)
             nc.vector.quantize_mx(
-                out=xc[i][:].bitcast(FP8X4),
-                scales=xs[i][:],
-                in_=xg[i][:].rearrange("p g r t -> p (g r t)"),
+                out=xc[j][:].rearrange("p g m -> p (g m)").bitcast(FP8X4),
+                scales=xs[j][:].rearrange("p g m -> p (g m)"),
+                in_=xg[j][:].rearrange("p g m t -> p (g m t)"),
             )
 
         wg = {}
@@ -212,8 +212,8 @@ def tile_selfattn_pa_kernel(
             for g in range(PASSES):
                 nc.tensor.matmul_mx(
                     out=acc[un][:],
-                    lhsT=xc[i][:, g * P : (g + 1) * P].bitcast(FP8X4),
-                    lhsT_scale=xs[i][:, g * P : (g + 1) * P],
+                    lhsT=xc[i // 2][:, g, (i % 2) * P : (i % 2 + 1) * P].bitcast(FP8X4),
+                    lhsT_scale=xs[i // 2][:, g, (i % 2) * P : (i % 2 + 1) * P],
                     rhs=wc[nb][:, g, :].bitcast(FP8X4),
                     rhs_scale=ws[nb][:, g, :],
                     start=(g == 0),
@@ -263,16 +263,19 @@ def tile_selfattn_pa_kernel(
                 fn(arg)
             deferred.clear()
 
-        def xprep(i):
-            if i >= NT:
+        def xprep(j, g):
+            if j >= NT // 2:
                 return
-            cast(i)
-            turn(i)
-            if i in SC_TILES:
-                scale_on_scalar(i)
+            if g == 0:
+                cast(2 * j)
+                cast(2 * j + 1)
+                turn(j)
+            if j in SC_PAIRS:
+                scale_on_scalar(j, g)
             else:
-                scale(i)
-            deferred.append((quant, i))
+                scale(j, g)
+            if g == PASSES - 1:
+                deferred.append((quant, j))
 
         def unit(un):
             mm(un)
@@ -291,21 +294,21 @@ def tile_selfattn_pa_kernel(
         turn(0)
         wcopy(0, 0, 0, VSH, True)
         wcopy(0, 0, VSH, NB, False)
-        scale(0)
+        scale(0, 0)
         wcopy(0, 1, 0, VSH, True)
         wcopy(0, 1, VSH, NB, False)
+        scale(0, 1)
         wquant(0, 0)
         quant(0)
         wquant(0, 1)
         cast(2)
+        cast(3)
         turn(1)
         for tt in range(4):
             negate(tq[tt], nc.gpsimd)
-        scale(1)
+        scale(1, 0)
+        scale(1, 1)
         quant(1)
-        turn(2)
-        scale(2)
-        quant(2)
 
         later = [(1, 0), (1, 1), (2, 0), (2, 1), (3, 0), (3, 1)]
         ready = [0]
@@ -321,7 +324,7 @@ def tile_selfattn_pa_kernel(
             if i == 2:
                 for tt in range(4):
                     negate(tk[tt], nc.vector)
-            xprep(i + 3)
+            xprep(i // 2 + 2, i % 2)
             order = [0, 1, 2, 3]
             if i == NT - 1:
                 order = [3, 0, 1, 2]

@@ -11,6 +11,7 @@ FP8 = mybir.dt.float8_e4m3fn
 FP8X4 = mybir.dt.float8_e4m3fn_x4
 MULT = mybir.AluOpType.mult
 ADD = mybir.AluOpType.add
+SUB = mybir.AluOpType.subtract
 
 P = 128
 TOKENS = 2048
@@ -21,9 +22,8 @@ NB = 512
 PAIRS = NB // 2
 FLOPS = 2 * TOKENS * K * 2048
 
-VSH = 384
 SC_PAIRS = (4, 5, 6, 7)
-VADD = ((3, 2), (6, 2), (9, 2), (12, 2), (15, 1), (15, 2))
+VADD = ((3, 2), (6, 2), (9, 2), (12, 2), (15, 2))
 COPY = mybir.ActivationFunctionType.Copy
 
 
@@ -44,7 +44,9 @@ def tile_selfattn_pa_kernel(
         xgp = ctx.enter_context(tc.tile_pool(name="xgp", bufs=2))
         xpp = ctx.enter_context(tc.tile_pool(name="xpp", bufs=2))
         wgp = ctx.enter_context(tc.tile_pool(name="wgp", bufs=2))
-        rp = ctx.enter_context(tc.tile_pool(name="rp", bufs=6))
+        rp = ctx.enter_context(tc.tile_pool(name="rp", bufs=4))
+        qp = ctx.enter_context(tc.tile_pool(name="qp", bufs=6))
+        kp = ctx.enter_context(tc.tile_pool(name="kp", bufs=4))
         vp = ctx.enter_context(tc.tile_pool(name="vp", bufs=4))
         pst = ctx.enter_context(tc.psum_pool(name="pst", bufs=2))
         psa = ctx.enter_context(tc.psum_pool(name="psa", bufs=6))
@@ -60,12 +62,14 @@ def tile_selfattn_pa_kernel(
         wraw = []
         tq = []
         tk = []
+        td = []
         for j in range(NT // 2):
             xb.append(keep.tile([P, 2, K], U8, name="xb%d" % j))
         for nb in range(4):
             wraw.append(keep.tile([P, PASSES, 4, NB], BF16, name="wraw%d" % nb))
         for tt in range(4):
-            tq.append(keep.tile([P, 4, 2 * PAIRS], BF16, name="tq%d" % tt))
+            tq.append(keep.tile([P, 2, 2 * PAIRS], BF16, name="tq%d" % tt))
+            td.append(keep.tile([P, 2, 2 * PAIRS], F32, name="td%d" % tt))
             tk.append(keep.tile([P, 4, PAIRS], BF16, name="tk%d" % tt))
 
         def load_x(j):
@@ -82,7 +86,7 @@ def tile_selfattn_pa_kernel(
                 )
 
         def load_tq(tt):
-            nc.sync.dma_start(out=tq[tt][:, 2, :], in_=sin_q[tt * P : (tt + 1) * P, :])
+            nc.sync.dma_start(out=tq[tt][:, 1, :], in_=sin_q[tt * P : (tt + 1) * P, :])
             nc.sync.dma_start(out=tq[tt][:, 0, :], in_=cos_q[tt * P : (tt + 1) * P, :])
 
         def load_tk(tt):
@@ -105,6 +109,12 @@ def tile_selfattn_pa_kernel(
         load_w(3)
         for j in range(4, NT // 2):
             load_x(j)
+
+        def sumdiff(tt, eng):
+            for e, op in ((0, SUB), (1, ADD)):
+                eng.tensor_tensor(
+                    out=td[tt][:, e, :], in0=tq[tt][:, 0, :], in1=tq[tt][:, 1, :], op=op
+                )
 
         def negate(t, eng):
             eng.tensor_scalar(
@@ -190,7 +200,12 @@ def tile_selfattn_pa_kernel(
             if nb not in wg:
                 wg[nb] = wgp.tile([P, PASSES, NB, 4], BF16, name="wg", align_bytes=64)
             dst = wg[nb][:, g, c0:c1, :]
-            src = wraw[nb][:, g, :, c0:c1].rearrange("p j n -> p n j")
+            if nb < 2:
+                e, i0 = divmod(c0, PAIRS)
+                first = 2 * i0 + 1 - e
+                src = wraw[nb][:, g, :, first : first + 2 * (c1 - c0) - 1 : 2].rearrange("p j n -> p n j")
+            else:
+                src = wraw[nb][:, g, :, c0:c1].rearrange("p j n -> p n j")
             if on_vector:
                 nc.vector.tensor_copy(out=dst, in_=src)
             else:
@@ -220,11 +235,28 @@ def tile_selfattn_pa_kernel(
                     stop=(g == PASSES - 1),
                 )
 
+        ysum = {}
+        k1 = {}
+
+        def mm_sum(i, nbs):
+            ysum[i] = psa.tile([P, 2, PAIRS], F32, name="acc")
+            for nb in nbs:
+                for g in range(PASSES):
+                    for e in range(2):
+                        cols = slice(e * PAIRS, (e + 1) * PAIRS)
+                        nc.tensor.matmul_mx(
+                            out=ysum[i][:, nb, :],
+                            lhsT=xc[i // 2][:, g, (i % 2) * P : (i % 2 + 1) * P].bitcast(FP8X4),
+                            lhsT_scale=xs[i // 2][:, g, (i % 2) * P : (i % 2 + 1) * P],
+                            rhs=wc[nb][:, g, cols].bitcast(FP8X4),
+                            rhs_scale=ws[nb][:, g, cols],
+                            start=(g == 0 and e == 0),
+                            stop=(g == PASSES - 1 and e == 1),
+                        )
+
         def table(un):
             i, nb = un
-            if nb == 2:
-                return tk[i % 4][:, :, :]
-            return tq[i % 4][:, :, nb * PAIRS : (nb + 1) * PAIRS]
+            return tk[i % 4][:, :, :]
 
         def rope_products(un):
             xy[un] = rp.tile([P, 2, PAIRS, 2], F32, name="rxy")
@@ -237,6 +269,39 @@ def tile_selfattn_pa_kernel(
                 in1=table(un).rearrange("p (e h) i -> p e i h", e=2),
                 op=MULT,
             )
+
+        def sum_product(i, nbs):
+            n0, n1 = nbs[0], nbs[-1] + 1
+            k1[i] = kp.tile([P, 2, PAIRS], F32, name="k1")
+            nc.vector.tensor_tensor(
+                out=k1[i][:, n0:n1, :],
+                in0=ysum[i][:, n0:n1, :],
+                in1=tq[i % 4][:, 0, n0 * PAIRS : n1 * PAIRS].rearrange("p (b i) -> p b i", i=PAIRS),
+                op=MULT,
+            )
+
+        def odd_even_products(un):
+            i, nb = un
+            xy[un] = qp.tile([P, PAIRS, 2], F32, name="qxy")
+            nc.vector.tensor_tensor(
+                out=xy[un][:],
+                in0=acc[un][:].rearrange("p (e i) -> p i e", e=2),
+                in1=td[i % 4][:, :, nb * PAIRS : (nb + 1) * PAIRS].rearrange("p e i -> p i e"),
+                op=MULT,
+            )
+
+        def finish_q(un):
+            i, nb = un
+            eng = nc.gpsimd
+            if un in VADD:
+                eng = nc.vector
+            eng.tensor_tensor(
+                out=xy[un][:],
+                in0=k1[i][:, nb, :].unsqueeze(2).to_broadcast([P, PAIRS, 2]),
+                in1=xy[un][:],
+                op=SUB,
+            )
+            store(un, xy[un][:].rearrange("p i e -> p (i e)"))
 
         def store(un, src):
             i, nb = un
@@ -277,6 +342,17 @@ def tile_selfattn_pa_kernel(
             if g == PASSES - 1:
                 deferred.append((quant, j))
 
+        def qunit(i, nbs):
+            mm_sum(i, nbs)
+            for nb in nbs:
+                mm((i, nb))
+            sum_product(i, nbs)
+            for nb in nbs:
+                un = (i, nb)
+                odd_even_products(un)
+                flush()
+                finish_q(un)
+
         def unit(un):
             mm(un)
             if un[1] == 3:
@@ -292,11 +368,13 @@ def tile_selfattn_pa_kernel(
         cast(0)
         cast(1)
         turn(0)
-        wcopy(0, 0, 0, VSH, True)
-        wcopy(0, 0, VSH, NB, False)
+        wcopy(0, 0, 0, PAIRS, True)
+        wcopy(0, 0, PAIRS, PAIRS + PAIRS // 2, True)
+        wcopy(0, 0, PAIRS + PAIRS // 2, NB, False)
         scale(0, 0)
-        wcopy(0, 1, 0, VSH, True)
-        wcopy(0, 1, VSH, NB, False)
+        wcopy(0, 1, 0, PAIRS, True)
+        wcopy(0, 1, PAIRS, PAIRS + PAIRS // 2, True)
+        wcopy(0, 1, PAIRS + PAIRS // 2, NB, False)
         scale(0, 1)
         wquant(0, 0)
         quant(0)
@@ -305,7 +383,7 @@ def tile_selfattn_pa_kernel(
         cast(3)
         turn(1)
         for tt in range(4):
-            negate(tq[tt], nc.gpsimd)
+            sumdiff(tt, nc.gpsimd)
         scale(1, 0)
         scale(1, 1)
         quant(1)
@@ -329,7 +407,16 @@ def tile_selfattn_pa_kernel(
             if i == NT - 1:
                 order = [3, 0, 1, 2]
             for j in range(i + 1):
+                nbs = []
+                for nb in (0, 1):
+                    if nb in ready and (j, nb) not in done:
+                        nbs.append(nb)
                 for nb in order:
+                    if nb in nbs:
+                        if nb == nbs[0]:
+                            qunit(j, nbs)
+                        done.add((j, nb))
+                        continue
                     if nb in ready and (j, nb) not in done:
                         done.add((j, nb))
                         unit((j, nb))

@@ -23,7 +23,14 @@ PAIRS = NB // 2
 FLOPS = 2 * TOKENS * K * 2048
 
 SC_PAIRS = (4, 5, 6, 7)
-VADD = ((3, 2), (6, 2), (9, 2), (12, 2), (15, 2))
+VADD = ((3, 2), (6, 2), (9, 2), (12, 2), (15, 1), (15, 2))
+THREE = (0,)
+PREP = {2: 0, 3: 2, 4: 4, 5: 6, 6: 8, 7: 10}
+WPREP = {(1, 0): 0, (1, 1): 1, (2, 0): 2, (2, 1): 3, (3, 0): 4, (3, 1): 5}
+TABENG = ("g", "g", "g", "g")
+KTAB = 2
+BUFR, BUFQ, BUFK, BUFV = 6, 6, 4, 4
+W0 = ((0, 256, True), (256, 384, True), (384, 512, False))
 COPY = mybir.ActivationFunctionType.Copy
 
 
@@ -44,10 +51,10 @@ def tile_selfattn_pa_kernel(
         xgp = ctx.enter_context(tc.tile_pool(name="xgp", bufs=2))
         xpp = ctx.enter_context(tc.tile_pool(name="xpp", bufs=2))
         wgp = ctx.enter_context(tc.tile_pool(name="wgp", bufs=2))
-        rp = ctx.enter_context(tc.tile_pool(name="rp", bufs=4))
-        qp = ctx.enter_context(tc.tile_pool(name="qp", bufs=6))
-        kp = ctx.enter_context(tc.tile_pool(name="kp", bufs=4))
-        vp = ctx.enter_context(tc.tile_pool(name="vp", bufs=4))
+        rp = ctx.enter_context(tc.tile_pool(name="rp", bufs=BUFR))
+        qp = ctx.enter_context(tc.tile_pool(name="qp", bufs=BUFQ))
+        kp = ctx.enter_context(tc.tile_pool(name="kp", bufs=BUFK))
+        vp = ctx.enter_context(tc.tile_pool(name="vp", bufs=BUFV))
         pst = ctx.enter_context(tc.psum_pool(name="pst", bufs=2))
         psa = ctx.enter_context(tc.psum_pool(name="psa", bufs=6))
 
@@ -68,8 +75,8 @@ def tile_selfattn_pa_kernel(
         for nb in range(4):
             wraw.append(keep.tile([P, PASSES, 4, NB], BF16, name="wraw%d" % nb))
         for tt in range(4):
-            tq.append(keep.tile([P, 2, 2 * PAIRS], BF16, name="tq%d" % tt))
-            td.append(keep.tile([P, 2, 2 * PAIRS], F32, name="td%d" % tt))
+            tq.append(keep.tile([P, 4, 2 * PAIRS], BF16, name="tq%d" % tt))
+            td.append(keep.tile([P, 2, PAIRS], F32, name="td%d" % tt))
             tk.append(keep.tile([P, 4, PAIRS], BF16, name="tk%d" % tt))
 
         def load_x(j):
@@ -86,7 +93,7 @@ def tile_selfattn_pa_kernel(
                 )
 
         def load_tq(tt):
-            nc.sync.dma_start(out=tq[tt][:, 1, :], in_=sin_q[tt * P : (tt + 1) * P, :])
+            nc.sync.dma_start(out=tq[tt][:, 2, :], in_=sin_q[tt * P : (tt + 1) * P, :])
             nc.sync.dma_start(out=tq[tt][:, 0, :], in_=cos_q[tt * P : (tt + 1) * P, :])
 
         def load_tk(tt):
@@ -113,8 +120,22 @@ def tile_selfattn_pa_kernel(
         def sumdiff(tt, eng):
             for e, op in ((0, SUB), (1, ADD)):
                 eng.tensor_tensor(
-                    out=td[tt][:, e, :], in0=tq[tt][:, 0, :], in1=tq[tt][:, 1, :], op=op
+                    out=td[tt][:, e, :], in0=tq[tt][:, 0, :PAIRS], in1=tq[tt][:, 2, :PAIRS], op=op
                 )
+
+        def qtables(tt):
+            eng = nc.gpsimd if TABENG[tt] == "g" else nc.vector
+            if 0 in THREE:
+                sumdiff(tt, eng)
+                c = slice(PAIRS, 2 * PAIRS)
+            else:
+                c = slice(0, 2 * PAIRS)
+            eng.tensor_scalar(
+                out=tq[tt][:, 1, c], in0=tq[tt][:, 2, c], scalar1=-1.0, scalar2=0.0, op0=MULT, op1=ADD
+            )
+            eng.tensor_scalar(
+                out=tq[tt][:, 3, c], in0=tq[tt][:, 0, c], scalar1=1.0, scalar2=0.0, op0=MULT, op1=ADD
+            )
 
         def negate(t, eng):
             eng.tensor_scalar(
@@ -200,7 +221,7 @@ def tile_selfattn_pa_kernel(
             if nb not in wg:
                 wg[nb] = wgp.tile([P, PASSES, NB, 4], BF16, name="wg", align_bytes=64)
             dst = wg[nb][:, g, c0:c1, :]
-            if nb < 2:
+            if nb in THREE:
                 e, i0 = divmod(c0, PAIRS)
                 first = 2 * i0 + 1 - e
                 src = wraw[nb][:, g, :, first : first + 2 * (c1 - c0) - 1 : 2].rearrange("p j n -> p n j")
@@ -238,25 +259,41 @@ def tile_selfattn_pa_kernel(
         ysum = {}
         k1 = {}
 
-        def mm_sum(i, nbs):
-            ysum[i] = psa.tile([P, 2, PAIRS], F32, name="acc")
-            for nb in nbs:
-                for g in range(PASSES):
-                    for e in range(2):
-                        cols = slice(e * PAIRS, (e + 1) * PAIRS)
-                        nc.tensor.matmul_mx(
-                            out=ysum[i][:, nb, :],
-                            lhsT=xc[i // 2][:, g, (i % 2) * P : (i % 2 + 1) * P].bitcast(FP8X4),
-                            lhsT_scale=xs[i // 2][:, g, (i % 2) * P : (i % 2 + 1) * P],
-                            rhs=wc[nb][:, g, cols].bitcast(FP8X4),
-                            rhs_scale=ws[nb][:, g, cols],
-                            start=(g == 0 and e == 0),
-                            stop=(g == PASSES - 1 and e == 1),
-                        )
+        def mm_sum(un):
+            i, nb = un
+            ysum[un] = psa.tile([P, PAIRS], F32, name="acc")
+            for g in range(PASSES):
+                for e in range(2):
+                    cols = slice(e * PAIRS, (e + 1) * PAIRS)
+                    nc.tensor.matmul_mx(
+                        out=ysum[un][:],
+                        lhsT=xc[i // 2][:, g, (i % 2) * P : (i % 2 + 1) * P].bitcast(FP8X4),
+                        lhsT_scale=xs[i // 2][:, g, (i % 2) * P : (i % 2 + 1) * P],
+                        rhs=wc[nb][:, g, cols].bitcast(FP8X4),
+                        rhs_scale=ws[nb][:, g, cols],
+                        start=(g == 0 and e == 0),
+                        stop=(g == PASSES - 1 and e == 1),
+                    )
+
+        def three_products(un):
+            i, nb = un
+            k1[un] = kp.tile([P, PAIRS], F32, name="k1")
+            nc.vector.tensor_tensor(
+                out=k1[un][:], in0=ysum[un][:], in1=tq[i % 4][:, 0, :PAIRS], op=MULT
+            )
+            xy[un] = qp.tile([P, PAIRS, 2], F32, name="qxy")
+            nc.vector.tensor_tensor(
+                out=xy[un][:],
+                in0=acc[un][:].rearrange("p (e i) -> p i e", e=2),
+                in1=td[i % 4][:].rearrange("p e i -> p i e"),
+                op=MULT,
+            )
 
         def table(un):
             i, nb = un
-            return tk[i % 4][:, :, :]
+            if nb == 2:
+                return tk[i % 4][:, :, :]
+            return tq[i % 4][:, :, nb * PAIRS : (nb + 1) * PAIRS]
 
         def rope_products(un):
             xy[un] = rp.tile([P, 2, PAIRS, 2], F32, name="rxy")
@@ -270,49 +307,25 @@ def tile_selfattn_pa_kernel(
                 op=MULT,
             )
 
-        def sum_product(i, nbs):
-            n0, n1 = nbs[0], nbs[-1] + 1
-            k1[i] = kp.tile([P, 2, PAIRS], F32, name="k1")
-            nc.vector.tensor_tensor(
-                out=k1[i][:, n0:n1, :],
-                in0=ysum[i][:, n0:n1, :],
-                in1=tq[i % 4][:, 0, n0 * PAIRS : n1 * PAIRS].rearrange("p (b i) -> p b i", i=PAIRS),
-                op=MULT,
-            )
-
-        def odd_even_products(un):
-            i, nb = un
-            xy[un] = qp.tile([P, PAIRS, 2], F32, name="qxy")
-            nc.vector.tensor_tensor(
-                out=xy[un][:],
-                in0=acc[un][:].rearrange("p (e i) -> p i e", e=2),
-                in1=td[i % 4][:, :, nb * PAIRS : (nb + 1) * PAIRS].rearrange("p e i -> p i e"),
-                op=MULT,
-            )
-
-        def finish_q(un):
-            i, nb = un
-            eng = nc.gpsimd
-            if un in VADD:
-                eng = nc.vector
-            eng.tensor_tensor(
-                out=xy[un][:],
-                in0=k1[i][:, nb, :].unsqueeze(2).to_broadcast([P, PAIRS, 2]),
-                in1=xy[un][:],
-                op=SUB,
-            )
-            store(un, xy[un][:].rearrange("p i e -> p (i e)"))
-
         def store(un, src):
             i, nb = un
             nc.sync.dma_start(out=o_dst[nb][i * P : (i + 1) * P, :], in_=src)
 
         def finish(un):
-            a = xy[un][:, 0]
-            b = xy[un][:, 1]
             eng = nc.gpsimd
             if un in VADD:
                 eng = nc.vector
+            if un[1] in THREE:
+                eng.tensor_tensor(
+                    out=xy[un][:],
+                    in0=k1[un][:].unsqueeze(2).to_broadcast([P, PAIRS, 2]),
+                    in1=xy[un][:],
+                    op=SUB,
+                )
+                store(un, xy[un][:].rearrange("p i e -> p (i e)"))
+                return
+            a = xy[un][:, 0]
+            b = xy[un][:, 1]
             eng.tensor_tensor(out=a, in0=a, in1=b, op=ADD)
             store(un, a.rearrange("p i e -> p (i e)"))
 
@@ -342,23 +355,17 @@ def tile_selfattn_pa_kernel(
             if g == PASSES - 1:
                 deferred.append((quant, j))
 
-        def qunit(i, nbs):
-            mm_sum(i, nbs)
-            for nb in nbs:
-                mm((i, nb))
-            sum_product(i, nbs)
-            for nb in nbs:
-                un = (i, nb)
-                odd_even_products(un)
-                flush()
-                finish_q(un)
-
         def unit(un):
             mm(un)
+            if un[1] in THREE:
+                mm_sum(un)
             if un[1] == 3:
                 vcopy(un)
                 return
-            rope_products(un)
+            if un[1] in THREE:
+                three_products(un)
+            else:
+                rope_products(un)
             flush()
             if un in VADD:
                 deferred.append((finish, un))
@@ -368,14 +375,10 @@ def tile_selfattn_pa_kernel(
         cast(0)
         cast(1)
         turn(0)
-        wcopy(0, 0, 0, PAIRS, True)
-        wcopy(0, 0, PAIRS, PAIRS + PAIRS // 2, True)
-        wcopy(0, 0, PAIRS + PAIRS // 2, NB, False)
-        scale(0, 0)
-        wcopy(0, 1, 0, PAIRS, True)
-        wcopy(0, 1, PAIRS, PAIRS + PAIRS // 2, True)
-        wcopy(0, 1, PAIRS + PAIRS // 2, NB, False)
-        scale(0, 1)
+        for g in range(PASSES):
+            for c0, c1, v in W0:
+                wcopy(0, g, c0, c1, v)
+            scale(0, g)
         wquant(0, 0)
         quant(0)
         wquant(0, 1)
@@ -383,40 +386,38 @@ def tile_selfattn_pa_kernel(
         cast(3)
         turn(1)
         for tt in range(4):
-            sumdiff(tt, nc.gpsimd)
-        scale(1, 0)
-        scale(1, 1)
+            qtables(tt)
+        if 1 in SC_PAIRS:
+            scale_on_scalar(1, 0)
+            scale_on_scalar(1, 1)
+        else:
+            scale(1, 0)
+            scale(1, 1)
         quant(1)
 
-        later = [(1, 0), (1, 1), (2, 0), (2, 1), (3, 0), (3, 1)]
         ready = [0]
         done = set()
         for i in range(NT):
-            if i < len(later):
-                nb, g = later[i]
-                wcopy(nb, g, 0, NB // 2, False)
-                wcopy(nb, g, NB // 2, NB, False)
-                wquant(nb, g)
-                if g == PASSES - 1:
-                    ready.append(nb)
-            if i == 2:
+            for nb in range(1, 4):
+                for g in range(PASSES):
+                    if WPREP[nb, g] == i:
+                        wcopy(nb, g, 0, NB // 2, False)
+                        wcopy(nb, g, NB // 2, NB, False)
+                        wquant(nb, g)
+                        if g == PASSES - 1:
+                            ready.append(nb)
+            if i == KTAB:
                 for tt in range(4):
                     negate(tk[tt], nc.vector)
-            xprep(i // 2 + 2, i % 2)
+            for j in range(2, NT // 2):
+                for g in range(PASSES):
+                    if PREP[j] + g == i:
+                        xprep(j, g)
             order = [0, 1, 2, 3]
             if i == NT - 1:
                 order = [3, 0, 1, 2]
             for j in range(i + 1):
-                nbs = []
-                for nb in (0, 1):
-                    if nb in ready and (j, nb) not in done:
-                        nbs.append(nb)
                 for nb in order:
-                    if nb in nbs:
-                        if nb == nbs[0]:
-                            qunit(j, nbs)
-                        done.add((j, nb))
-                        continue
                     if nb in ready and (j, nb) not in done:
                         done.add((j, nb))
                         unit((j, nb))

@@ -23,12 +23,15 @@ PAIRS = NB // 2
 FLOPS = 2 * TOKENS * K * 2048
 
 SC_PAIRS = (4, 5, 6, 7)
-VADD = ((3, 2), (6, 2), (9, 2), (12, 2), (15, 1), (15, 2))
+VADD = ((6, 2), (7, 2), (8, 2), (9, 2), (10, 2), (11, 2), (12, 2), (13, 2), (14, 2), (15, 2), (15, 1))
 THREE = (0,)
 PREP = {2: 0, 3: 2, 4: 4, 5: 6, 6: 8, 7: 10}
 WPREP = {(1, 0): 0, (1, 1): 1, (2, 0): 2, (2, 1): 3, (3, 0): 4, (3, 1): 5}
-TABENG = ("g", "g", "g", "g")
+TABENG = ("g", "g", "v", "v")
 KTAB = 2
+QTAB = (-1, -1, 1, 2)
+WQ2 = False
+QUADS = False
 BUFR, BUFQ, BUFK, BUFV = 6, 6, 4, 4
 W0 = ((0, 256, True), (256, 384, True), (384, 512, False))
 COPY = mybir.ActivationFunctionType.Copy
@@ -68,7 +71,7 @@ def tile_selfattn_pa_kernel(
         xb = []
         wraw = []
         tq = []
-        tk = []
+        tk = keep.tile([P, 4, 4, PAIRS], BF16, name="tk")
         td = []
         for j in range(NT // 2):
             xb.append(keep.tile([P, 2, K], U8, name="xb%d" % j))
@@ -77,7 +80,6 @@ def tile_selfattn_pa_kernel(
         for tt in range(4):
             tq.append(keep.tile([P, 4, 2 * PAIRS], BF16, name="tq%d" % tt))
             td.append(keep.tile([P, 2, PAIRS], F32, name="td%d" % tt))
-            tk.append(keep.tile([P, 4, PAIRS], BF16, name="tk%d" % tt))
 
         def load_x(j):
             nc.sync.dma_start(
@@ -97,8 +99,8 @@ def tile_selfattn_pa_kernel(
             nc.sync.dma_start(out=tq[tt][:, 0, :], in_=cos_q[tt * P : (tt + 1) * P, :])
 
         def load_tk(tt):
-            nc.sync.dma_start(out=tk[tt][:, 2, :], in_=sin_k[tt * P : (tt + 1) * P, :])
-            nc.sync.dma_start(out=tk[tt][:, 0, :], in_=cos_k[tt * P : (tt + 1) * P, :])
+            nc.sync.dma_start(out=tk[:, 2, tt, :], in_=sin_k[tt * P : (tt + 1) * P, :])
+            nc.sync.dma_start(out=tk[:, 0, tt, :], in_=cos_k[tt * P : (tt + 1) * P, :])
 
         load_x(0)
         load_w(0)
@@ -130,20 +132,20 @@ def tile_selfattn_pa_kernel(
                 c = slice(PAIRS, 2 * PAIRS)
             else:
                 c = slice(0, 2 * PAIRS)
-            eng.tensor_scalar(
-                out=tq[tt][:, 1, c], in0=tq[tt][:, 2, c], scalar1=-1.0, scalar2=0.0, op0=MULT, op1=ADD
-            )
-            eng.tensor_scalar(
-                out=tq[tt][:, 3, c], in0=tq[tt][:, 0, c], scalar1=1.0, scalar2=0.0, op0=MULT, op1=ADD
-            )
+            if TABENG[tt] == "g":
+                eng.tensor_scalar(
+                    out=tq[tt][:, 1, c], in0=tq[tt][:, 2, c], scalar1=-1.0, scalar2=0.0, op0=MULT, op1=ADD
+                )
+                eng.tensor_scalar(
+                    out=tq[tt][:, 3, c], in0=tq[tt][:, 0, c], scalar1=1.0, scalar2=0.0, op0=MULT, op1=ADD
+                )
+            else:
+                eng.tensor_scalar(out=tq[tt][:, 1, c], in0=tq[tt][:, 2, c], scalar1=-1.0, scalar2=None, op0=MULT)
+                eng.tensor_copy(out=tq[tt][:, 3, c], in_=tq[tt][:, 0, c])
 
-        def negate(t, eng):
-            eng.tensor_scalar(
-                out=t[:, 1, :], in0=t[:, 2, :], scalar1=-1.0, scalar2=0.0, op0=MULT, op1=ADD
-            )
-            eng.tensor_scalar(
-                out=t[:, 3, :], in0=t[:, 0, :], scalar1=1.0, scalar2=0.0, op0=MULT, op1=ADD
-            )
+        def ktables():
+            nc.vector.tensor_scalar(out=tk[:, 1], in0=tk[:, 2], scalar1=-1.0, scalar2=None, op0=MULT)
+            nc.vector.tensor_copy(out=tk[:, 3], in_=tk[:, 0])
 
         xbf = {}
         xt = {}
@@ -151,6 +153,13 @@ def tile_selfattn_pa_kernel(
         xc = {}
         xs = {}
         xpl = {}
+
+        def quad(j):
+            return j if j < 2 or not QUADS else 1 + j // 2
+
+        def pairs_of(q):
+            return (q,) if q < 2 or not QUADS else (2 * q - 2, 2 * q - 1)
+
 
         def cast(i):
             j, n = divmod(i, 2)
@@ -171,11 +180,16 @@ def tile_selfattn_pa_kernel(
         def halfwords(j, g):
             return xt[(j, g)][:].rearrange("p u n r -> p u (n r)").bitcast(BF16)
 
+        def staging(j):
+            q = quad(j)
+            if q not in xg:
+                n = len(pairs_of(q))
+                xg[q] = xgp.tile([P, n, PASSES, 2 * P, 4], BF16, name="xg%d" % n, align_bytes=64)
+            return xg[q][:, j - pairs_of(q)[0]]
+
         def scale(j, g):
-            if g == 0:
-                xg[j] = xgp.tile([P, PASSES, 2 * P, 4], BF16, name="xg", align_bytes=64)
             nc.vector.tensor_tensor(
-                out=xg[j][:, g].rearrange("p m (u e) -> p m u e", u=2),
+                out=staging(j)[:, g].rearrange("p m (u e) -> p m u e", u=2),
                 in0=halfwords(j, g).rearrange("p u (m e) -> p m u e", e=2),
                 in1=sk[:, g, :]
                 .rearrange("p (u e) -> p u e", u=2)
@@ -198,17 +212,20 @@ def tile_selfattn_pa_kernel(
                         scale=sk[:, g, t : t + 1],
                     )
             if g == PASSES - 1:
-                xg[j] = xgp.tile([P, PASSES, 2 * P, 4], BF16, name="xg", align_bytes=64)
-                nc.scalar.copy(out=xg[j][:], in_=xpl[j][:].rearrange("p g t m -> p g m t"))
+                nc.scalar.copy(out=staging(j), in_=xpl[j][:].rearrange("p g t m -> p g m t"))
 
-        def quant(j):
-            xc[j] = keep.tile([P, PASSES, 2 * P], U32, name="xc%d" % j, align_bytes=64)
-            xs[j] = keep.tile([P, PASSES, 2 * P], U8, name="xs%d" % j, align_bytes=64)
+        def quant(q):
+            n = len(pairs_of(q))
+            codes = keep.tile([P, n, PASSES, 2 * P], U32, name="xc%d" % q, align_bytes=64)
+            scales = keep.tile([P, n, PASSES, 2 * P], U8, name="xs%d" % q, align_bytes=64)
             nc.vector.quantize_mx(
-                out=xc[j][:].rearrange("p g m -> p (g m)").bitcast(FP8X4),
-                scales=xs[j][:].rearrange("p g m -> p (g m)"),
-                in_=xg[j][:].rearrange("p g m t -> p (g m t)"),
+                out=codes[:].rearrange("p n g m -> p (n g m)").bitcast(FP8X4),
+                scales=scales[:].rearrange("p n g m -> p (n g m)"),
+                in_=xg[q][:].rearrange("p n g m t -> p (n g m t)"),
             )
+            for j in pairs_of(q):
+                xc[j] = codes[:, j - pairs_of(q)[0]]
+                xs[j] = scales[:, j - pairs_of(q)[0]]
 
         wg = {}
         wc = []
@@ -232,11 +249,11 @@ def tile_selfattn_pa_kernel(
             else:
                 nc.scalar.copy(out=dst, in_=src)
 
-        def wquant(nb, g):
+        def wquant(nb, g0, g1):
             nc.vector.quantize_mx(
-                out=wc[nb][:, g, :].bitcast(FP8X4),
-                scales=ws[nb][:, g, :],
-                in_=wg[nb][:, g].rearrange("p n j -> p (n j)"),
+                out=wc[nb][:, g0:g1, :].rearrange("p g n -> p (g n)").bitcast(FP8X4),
+                scales=ws[nb][:, g0:g1, :].rearrange("p g n -> p (g n)"),
+                in_=wg[nb][:, g0:g1].rearrange("p g n j -> p (g n j)"),
             )
 
         acc = {}
@@ -292,7 +309,7 @@ def tile_selfattn_pa_kernel(
         def table(un):
             i, nb = un
             if nb == 2:
-                return tk[i % 4][:, :, :]
+                return tk[:, :, i % 4, :]
             return tq[i % 4][:, :, nb * PAIRS : (nb + 1) * PAIRS]
 
         def rope_products(un):
@@ -353,7 +370,8 @@ def tile_selfattn_pa_kernel(
             else:
                 scale(j, g)
             if g == PASSES - 1:
-                deferred.append((quant, j))
+                if j == pairs_of(quad(j))[-1]:
+                    deferred.append((quant, quad(j)))
 
         def unit(un):
             mm(un)
@@ -379,14 +397,15 @@ def tile_selfattn_pa_kernel(
             for c0, c1, v in W0:
                 wcopy(0, g, c0, c1, v)
             scale(0, g)
-        wquant(0, 0)
+        wquant(0, 0, 1)
         quant(0)
-        wquant(0, 1)
+        wquant(0, 1, 2)
         cast(2)
         cast(3)
         turn(1)
         for tt in range(4):
-            qtables(tt)
+            if QTAB[tt] < 0:
+                qtables(tt)
         if 1 in SC_PAIRS:
             scale_on_scalar(1, 0)
             scale_on_scalar(1, 1)
@@ -403,12 +422,17 @@ def tile_selfattn_pa_kernel(
                     if WPREP[nb, g] == i:
                         wcopy(nb, g, 0, NB // 2, False)
                         wcopy(nb, g, NB // 2, NB, False)
-                        wquant(nb, g)
+                        if not WQ2:
+                            wquant(nb, g, g + 1)
+                        elif g == PASSES - 1:
+                            wquant(nb, 0, PASSES)
                         if g == PASSES - 1:
                             ready.append(nb)
+            for tt in range(4):
+                if QTAB[tt] == i:
+                    qtables(tt)
             if i == KTAB:
-                for tt in range(4):
-                    negate(tk[tt], nc.vector)
+                ktables()
             for j in range(2, NT // 2):
                 for g in range(PASSES):
                     if PREP[j] + g == i:

@@ -22,18 +22,27 @@ NB = 512
 PAIRS = NB // 2
 FLOPS = 2 * TOKENS * K * 2048
 
-SC_PAIRS = (4, 5, 6, 7)
+SC_PAIRS = (3, 5, 6, 7)
 VADD = ((6, 2), (7, 2), (8, 2), (9, 2), (10, 2), (11, 2), (12, 2), (13, 2), (14, 2), (15, 2), (15, 1))
 THREE = (0,)
-PREP = {2: 0, 3: 2, 4: 4, 5: 6, 6: 8, 7: 10}
+PREP = {2: 1, 3: 3, 4: 5, 5: 7, 6: 9, 7: 11}
 WPREP = {(1, 0): 0, (1, 1): 1, (2, 0): 2, (2, 1): 3, (3, 0): 4, (3, 1): 5}
-TABENG = ("g", "g", "v", "v")
-KTAB = 2
-QTAB = (-1, -1, 1, 2)
+TABENG = ("g", "v", "v", "v")
+KTAB = 1
+WPE = ()
+VCAST = (0, 1)
+WG = ()
+GHEAD = ()
+GSTEP = 128
+LOADS = ("x0", "w0", "q0", "q1", "x1", "w1", "q2", "q3", "x2", "w2", "x3", "k", "w3", "x4", "x5", "x6", "x7")
+QTAB = (0, 1, 2, 3)
 WQ2 = False
 QUADS = False
-BUFR, BUFQ, BUFK, BUFV = 6, 6, 4, 4
-W0 = ((0, 256, True), (256, 384, True), (384, 512, False))
+BUFR = 8
+BUFQ = 8
+BUFK = 4
+BUFV = 4
+W0 = ((0, 256, False), (256, 512, False))
 COPY = mybir.ActivationFunctionType.Copy
 
 
@@ -63,6 +72,9 @@ def tile_selfattn_pa_kernel(
 
         ident = keep.tile([P, P], F32, name="ident")
         make_identity(nc, ident[:])
+        plus = keep.tile([P, P], BF16, name="plus")
+        if len(WPE):
+            nc.vector.tensor_copy(out=plus[:], in_=ident[:])
 
         sk = keep.tile([P, PASSES, 4], F32, name="sk")
         nc.sync.dma_start(
@@ -102,22 +114,16 @@ def tile_selfattn_pa_kernel(
             nc.sync.dma_start(out=tk[:, 2, tt, :], in_=sin_k[tt * P : (tt + 1) * P, :])
             nc.sync.dma_start(out=tk[:, 0, tt, :], in_=cos_k[tt * P : (tt + 1) * P, :])
 
-        load_x(0)
-        load_w(0)
-        load_tq(0)
-        load_tq(1)
-        load_x(1)
-        load_w(1)
-        load_tq(2)
-        load_tq(3)
-        load_x(2)
-        load_w(2)
-        load_x(3)
-        for tt in range(4):
-            load_tk(tt)
-        load_w(3)
-        for j in range(4, NT // 2):
-            load_x(j)
+        for what in LOADS:
+            if what == "k":
+                for tt in range(4):
+                    load_tk(tt)
+            elif what[0] == "x":
+                load_x(int(what[1]))
+            elif what[0] == "w":
+                load_w(int(what[1]))
+            else:
+                load_tq(int(what[1]))
 
         def sumdiff(tt, eng):
             for e, op in ((0, SUB), (1, ADD)):
@@ -165,7 +171,10 @@ def tile_selfattn_pa_kernel(
             j, n = divmod(i, 2)
             if n == 0:
                 xbf[j] = xbfp.tile([P, 2, K], BF16, name="xbf")
-            nc.scalar.copy(out=xbf[j][:, n, :], in_=xb[j][:, n, :].bitcast(FP8))
+            if i in VCAST:
+                nc.vector.tensor_copy(out=xbf[j][:, n, :], in_=xb[j][:, n, :].bitcast(FP8))
+            else:
+                nc.scalar.copy(out=xbf[j][:, n, :], in_=xb[j][:, n, :].bitcast(FP8))
 
         def turn(j):
             for g in range(PASSES):
@@ -234,6 +243,16 @@ def tile_selfattn_pa_kernel(
             wc.append(keep.tile([P, PASSES, NB], U32, name="wc%d" % nb, align_bytes=64))
             ws.append(keep.tile([P, PASSES, NB], U8, name="ws%d" % nb, align_bytes=64))
 
+        def winter(nb, g, c0, c1):
+            if nb not in wg:
+                wg[nb] = wgp.tile([P, PASSES, NB, 4], BF16, name="wg", align_bytes=64)
+            bank = psa.tile([P, NB // 2, 4], BF16, name="acc")
+            for j in range(4):
+                nc.tensor.matmul(
+                    bank[:, :, j], lhsT=plus[:], rhs=wraw[nb][:, g, j, c0:c1], start=True, stop=True
+                )
+            nc.scalar.copy(out=wg[nb][:, g, c0:c1, :], in_=bank[:])
+
         def wcopy(nb, g, c0, c1, on_vector):
             if nb not in wg:
                 wg[nb] = wgp.tile([P, PASSES, NB, 4], BF16, name="wg", align_bytes=64)
@@ -244,7 +263,9 @@ def tile_selfattn_pa_kernel(
                 src = wraw[nb][:, g, :, first : first + 2 * (c1 - c0) - 1 : 2].rearrange("p j n -> p n j")
             else:
                 src = wraw[nb][:, g, :, c0:c1].rearrange("p j n -> p n j")
-            if on_vector:
+            if on_vector == "g":
+                nc.gpsimd.tensor_scalar(out=dst, in0=src, scalar1=1.0, scalar2=0.0, op0=MULT, op1=ADD)
+            elif on_vector:
                 nc.vector.tensor_copy(out=dst, in_=src)
             else:
                 nc.scalar.copy(out=dst, in_=src)
@@ -406,6 +427,10 @@ def tile_selfattn_pa_kernel(
         for tt in range(4):
             if QTAB[tt] < 0:
                 qtables(tt)
+        for nb in GHEAD:
+            for g in range(PASSES):
+                for c1 in range(0, NB, GSTEP):
+                    wcopy(nb, g, c1, c1 + GSTEP, "g")
         if 1 in SC_PAIRS:
             scale_on_scalar(1, 0)
             scale_on_scalar(1, 1)
@@ -420,8 +445,16 @@ def tile_selfattn_pa_kernel(
             for nb in range(1, 4):
                 for g in range(PASSES):
                     if WPREP[nb, g] == i:
-                        wcopy(nb, g, 0, NB // 2, False)
-                        wcopy(nb, g, NB // 2, NB, False)
+                        for c0 in (0, NB // 2):
+                            if nb in GHEAD:
+                                continue
+                            if (nb, g, c0) in WG:
+                                for c1 in range(c0, c0 + 256, 128):
+                                    wcopy(nb, g, c1, c1 + 128, "g")
+                            elif nb in WPE:
+                                winter(nb, g, c0, c0 + NB // 2)
+                            else:
+                                wcopy(nb, g, c0, c0 + NB // 2, False)
                         if not WQ2:
                             wquant(nb, g, g + 1)
                         elif g == PASSES - 1:

@@ -22,19 +22,28 @@ NB = 512
 PAIRS = NB // 2
 FLOPS = 2 * TOKENS * K * 2048
 
-SC_PAIRS = (3, 5, 6, 7)
-VADD = ((6, 2), (7, 2), (8, 2), (9, 2), (10, 2), (11, 2), (12, 2), (13, 2), (14, 2), (15, 2), (15, 1))
+SC_PAIRS = (4, 5, 6, 7)
+VADD = ((5, 2), (6, 2), (7, 2), (8, 2), (9, 2), (10, 2), (11, 2), (12, 2), (13, 2), (14, 2), (15, 2), (15, 1))
 THREE = (0,)
-PREP = {2: 1, 3: 3, 4: 5, 5: 7, 6: 9, 7: 11}
-WPREP = {(1, 0): 0, (1, 1): 1, (2, 0): 2, (2, 1): 3, (3, 0): 4, (3, 1): 5}
-TABENG = ("g", "v", "v", "v")
+T3 = (16, 16)
+PREP = {2: 0, 3: 3, 4: 6, 5: 8, 6: 10, 7: 12}
+WPREP = {(1, 0): 2, (1, 1): 2, (2, 0): 3, (2, 1): 5, (3, 0): 5, (3, 1): 5}
+TABENG = ("v", "v", "g", "g")
 KTAB = 1
+FAST = False
+WARM = 0
+EARLY = 0
+CATCH = 2
+JOIN = ()
+PIECES = 1
+PADD = ()
+JLAST = 14
 WPE = ()
 VCAST = (0, 1)
 WG = ()
 GHEAD = ()
 GSTEP = 128
-LOADS = ("x0", "w0", "q0", "q1", "x1", "w1", "q2", "q3", "x2", "w2", "x3", "k", "w3", "x4", "x5", "x6", "x7")
+LOADS = ("x0", "w0", "q0", "x1", "q1", "w1", "x2", "q2", "q3", "w2", "k", "x3", "w3", "x4", "x5", "x6", "x7")
 QTAB = (0, 1, 2, 3)
 WQ2 = False
 QUADS = False
@@ -66,15 +75,24 @@ def tile_selfattn_pa_kernel(
         rp = ctx.enter_context(tc.tile_pool(name="rp", bufs=BUFR))
         qp = ctx.enter_context(tc.tile_pool(name="qp", bufs=BUFQ))
         kp = ctx.enter_context(tc.tile_pool(name="kp", bufs=BUFK))
+        jp = ctx.enter_context(tc.tile_pool(name="jp", bufs=3))
         vp = ctx.enter_context(tc.tile_pool(name="vp", bufs=BUFV))
         pst = ctx.enter_context(tc.psum_pool(name="pst", bufs=2))
         psa = ctx.enter_context(tc.psum_pool(name="psa", bufs=6))
 
         ident = keep.tile([P, P], F32, name="ident")
         make_identity(nc, ident[:])
+        if len(PADD):
+            negi = keep.tile([P, P], F32, name="negi")
+            nc.gpsimd.tensor_scalar(out=negi[:], in0=ident[:], scalar1=-1.0, scalar2=0.0, op0=MULT, op1=ADD)
         plus = keep.tile([P, P], BF16, name="plus")
         if len(WPE):
             nc.vector.tensor_copy(out=plus[:], in_=ident[:])
+
+        CS, SS = (2, 0) if len(THREE) == 2 else (0, 2)
+
+        def is3(un):
+            return un[1] in THREE and un[0] < T3[un[1]]
 
         sk = keep.tile([P, PASSES, 4], F32, name="sk")
         nc.sync.dma_start(
@@ -91,7 +109,7 @@ def tile_selfattn_pa_kernel(
             wraw.append(keep.tile([P, PASSES, 4, NB], BF16, name="wraw%d" % nb))
         for tt in range(4):
             tq.append(keep.tile([P, 4, 2 * PAIRS], BF16, name="tq%d" % tt))
-            td.append(keep.tile([P, 2, PAIRS], F32, name="td%d" % tt))
+            td.append(keep.tile([P, 2, len(THREE) * PAIRS], F32, name="td%d" % tt))
 
         def load_x(j):
             nc.sync.dma_start(
@@ -107,8 +125,8 @@ def tile_selfattn_pa_kernel(
                 )
 
         def load_tq(tt):
-            nc.sync.dma_start(out=tq[tt][:, 2, :], in_=sin_q[tt * P : (tt + 1) * P, :])
-            nc.sync.dma_start(out=tq[tt][:, 0, :], in_=cos_q[tt * P : (tt + 1) * P, :])
+            nc.sync.dma_start(out=tq[tt][:, SS, :], in_=sin_q[tt * P : (tt + 1) * P, :])
+            nc.sync.dma_start(out=tq[tt][:, CS, :], in_=cos_q[tt * P : (tt + 1) * P, :])
 
         def load_tk(tt):
             nc.sync.dma_start(out=tk[:, 2, tt, :], in_=sin_k[tt * P : (tt + 1) * P, :])
@@ -126,28 +144,31 @@ def tile_selfattn_pa_kernel(
                 load_tq(int(what[1]))
 
         def sumdiff(tt, eng):
+            c = slice(0, len(THREE) * PAIRS)
             for e, op in ((0, SUB), (1, ADD)):
-                eng.tensor_tensor(
-                    out=td[tt][:, e, :], in0=tq[tt][:, 0, :PAIRS], in1=tq[tt][:, 2, :PAIRS], op=op
-                )
+                eng.tensor_tensor(out=td[tt][:, e, :], in0=tq[tt][:, CS, c], in1=tq[tt][:, SS, c], op=op)
 
         def qtables(tt):
             eng = nc.gpsimd if TABENG[tt] == "g" else nc.vector
-            if 0 in THREE:
+            if len(THREE):
                 sumdiff(tt, eng)
-                c = slice(PAIRS, 2 * PAIRS)
-            else:
-                c = slice(0, 2 * PAIRS)
+            b0, b1 = 2, 0
+            for nb in range(2):
+                if nb not in THREE or T3[nb] < NT:
+                    b0, b1 = min(b0, nb), nb + 1
+            if b0 >= b1:
+                return
+            c = slice(b0 * PAIRS, b1 * PAIRS)
             if TABENG[tt] == "g":
                 eng.tensor_scalar(
-                    out=tq[tt][:, 1, c], in0=tq[tt][:, 2, c], scalar1=-1.0, scalar2=0.0, op0=MULT, op1=ADD
+                    out=tq[tt][:, CS + 1, c], in0=tq[tt][:, SS, c], scalar1=-1.0, scalar2=0.0, op0=MULT, op1=ADD
                 )
                 eng.tensor_scalar(
-                    out=tq[tt][:, 3, c], in0=tq[tt][:, 0, c], scalar1=1.0, scalar2=0.0, op0=MULT, op1=ADD
+                    out=tq[tt][:, SS + 1, c], in0=tq[tt][:, CS, c], scalar1=1.0, scalar2=0.0, op0=MULT, op1=ADD
                 )
             else:
-                eng.tensor_scalar(out=tq[tt][:, 1, c], in0=tq[tt][:, 2, c], scalar1=-1.0, scalar2=None, op0=MULT)
-                eng.tensor_copy(out=tq[tt][:, 3, c], in_=tq[tt][:, 0, c])
+                eng.tensor_scalar(out=tq[tt][:, CS + 1, c], in0=tq[tt][:, SS, c], scalar1=-1.0, scalar2=None, op0=MULT)
+                eng.tensor_copy(out=tq[tt][:, SS + 1, c], in_=tq[tt][:, CS, c])
 
         def ktables():
             nc.vector.tensor_scalar(out=tk[:, 1], in0=tk[:, 2], scalar1=-1.0, scalar2=None, op0=MULT)
@@ -221,7 +242,14 @@ def tile_selfattn_pa_kernel(
                         scale=sk[:, g, t : t + 1],
                     )
             if g == PASSES - 1:
-                nc.scalar.copy(out=staging(j), in_=xpl[j][:].rearrange("p g t m -> p g m t"))
+                if FAST:
+                    for q in range(PASSES):
+                        nc.scalar.copy(
+                            out=staging(j)[:, q].rearrange("p (c i) t -> p c t i", i=4),
+                            in_=xpl[j][:, q].rearrange("p t (c i) -> p c t i", i=4),
+                        )
+                else:
+                    nc.scalar.copy(out=staging(j), in_=xpl[j][:].rearrange("p g t m -> p g m t"))
 
         def quant(q):
             n = len(pairs_of(q))
@@ -263,6 +291,9 @@ def tile_selfattn_pa_kernel(
                 src = wraw[nb][:, g, :, first : first + 2 * (c1 - c0) - 1 : 2].rearrange("p j n -> p n j")
             else:
                 src = wraw[nb][:, g, :, c0:c1].rearrange("p j n -> p n j")
+            if FAST:
+                dst = dst.rearrange("p (c i) t -> p c t i", i=4)
+                src = src.rearrange("p (c i) t -> p c t i", i=4)
             if on_vector == "g":
                 nc.gpsimd.tensor_scalar(out=dst, in0=src, scalar1=1.0, scalar2=0.0, op0=MULT, op1=ADD)
             elif on_vector:
@@ -299,12 +330,13 @@ def tile_selfattn_pa_kernel(
 
         def mm_sum(un):
             i, nb = un
-            ysum[un] = psa.tile([P, PAIRS], F32, name="acc")
+            if ysum.get(i) is None:
+                ysum[i] = psa.tile([P, 2, PAIRS], F32, name="acc")
             for g in range(PASSES):
                 for e in range(2):
                     cols = slice(e * PAIRS, (e + 1) * PAIRS)
                     nc.tensor.matmul_mx(
-                        out=ysum[un][:],
+                        out=ysum[i][:, nb, :],
                         lhsT=xc[i // 2][:, g, (i % 2) * P : (i % 2 + 1) * P].bitcast(FP8X4),
                         lhsT_scale=xs[i // 2][:, g, (i % 2) * P : (i % 2 + 1) * P],
                         rhs=wc[nb][:, g, cols].bitcast(FP8X4),
@@ -313,19 +345,51 @@ def tile_selfattn_pa_kernel(
                         stop=(g == PASSES - 1 and e == 1),
                     )
 
-        def three_products(un):
-            i, nb = un
-            k1[un] = kp.tile([P, PAIRS], F32, name="k1")
+        def sum_product(i, nbs):
+            n0, n1 = nbs[0], nbs[-1] + 1
+            if len(JOIN) and joined((i, nbs[0])):
+                if i % 2 == 0:
+                    k1j[i // 2] = kp.tile([P, 2, 2, PAIRS], F32, name="k1j")
+                k1[i] = k1j[i // 2][:, i % 2]
+            else:
+                k1[i] = kp.tile([P, 2, PAIRS], F32, name="k1")
             nc.vector.tensor_tensor(
-                out=k1[un][:], in0=ysum[un][:], in1=tq[i % 4][:, 0, :PAIRS], op=MULT
-            )
-            xy[un] = qp.tile([P, PAIRS, 2], F32, name="qxy")
-            nc.vector.tensor_tensor(
-                out=xy[un][:],
-                in0=acc[un][:].rearrange("p (e i) -> p i e", e=2),
-                in1=td[i % 4][:].rearrange("p e i -> p i e"),
+                out=k1[i][:, n0:n1, :],
+                in0=ysum[i][:, n0:n1, :],
+                in1=tq[i % 4][:, CS, n0 * PAIRS : n1 * PAIRS].rearrange("p (b i) -> p b i", i=PAIRS),
                 op=MULT,
             )
+
+        def three_products(un):
+            i, nb = un
+            if joined(un):
+                if i % 2 == 0:
+                    joint[(i // 2, nb)] = jp.tile([P, 2, PAIRS, 2], F32, name="jq%d" % nb)
+                dst = joint[(i // 2, nb)][:, i % 2]
+            else:
+                xy[un] = qp.tile([P, PAIRS, 2], F32, name="qxy")
+                dst = xy[un][:]
+            nc.vector.tensor_tensor(
+                out=dst,
+                in0=acc[un][:].rearrange("p (e i) -> p i e", e=2),
+                in1=td[i % 4][:, :, nb * PAIRS : (nb + 1) * PAIRS].rearrange("p e i -> p i e"),
+                op=MULT,
+            )
+
+        def qunit(i, nbs):
+            for nb in nbs:
+                mm((i, nb))
+                mm_sum((i, nb))
+            sum_product(i, nbs)
+            for nb in nbs:
+                un = (i, nb)
+                three_products(un)
+                flush()
+                if un in VADD:
+                    deferred.append((finish, un))
+                else:
+                    finish(un)
+            ysum[i] = None
 
         def table(un):
             i, nb = un
@@ -333,12 +397,25 @@ def tile_selfattn_pa_kernel(
                 return tk[:, :, i % 4, :]
             return tq[i % 4][:, :, nb * PAIRS : (nb + 1) * PAIRS]
 
+        joint = {}
+        k1j = {}
+
+        def joined(un):
+            return un[1] in JOIN and un[0] < JLAST and un not in VADD and (un[0] ^ 1, un[1]) not in VADD
+
         def rope_products(un):
-            xy[un] = rp.tile([P, 2, PAIRS, 2], F32, name="rxy")
+            if joined(un):
+                i, nb = un
+                if i % 2 == 0:
+                    joint[(i // 2, nb)] = jp.tile([P, 2, 2, PAIRS, 2], F32, name="jr%d" % nb)
+                dst = joint[(i // 2, nb)][:, i % 2]
+            else:
+                xy[un] = rp.tile([P, 2, PAIRS, 2], F32, name="rxy")
+                dst = xy[un][:]
             nc.vector.tensor_tensor(
-                out=xy[un][:],
+                out=dst,
                 in0=acc[un][:]
-                .rearrange("p (i e) -> p e i", e=2)
+                .rearrange("p (e i) -> p e i" if un[1] in THREE else "p (i e) -> p e i", e=2)
                 .unsqueeze(3)
                 .to_broadcast([P, 2, PAIRS, 2]),
                 in1=table(un).rearrange("p (e h) i -> p e i h", e=2),
@@ -353,18 +430,57 @@ def tile_selfattn_pa_kernel(
             eng = nc.gpsimd
             if un in VADD:
                 eng = nc.vector
-            if un[1] in THREE:
-                eng.tensor_tensor(
-                    out=xy[un][:],
-                    in0=k1[un][:].unsqueeze(2).to_broadcast([P, PAIRS, 2]),
-                    in1=xy[un][:],
-                    op=SUB,
+            if joined(un):
+                i, nb = un
+                if i % 2 == 0:
+                    return
+                t = joint[(i // 2, nb)]
+                if is3(un):
+                    eng.tensor_tensor(
+                        out=t[:],
+                        in0=k1j[i // 2][:, :, nb, :].unsqueeze(3).to_broadcast([P, 2, PAIRS, 2]),
+                        in1=t[:],
+                        op=SUB,
+                    )
+                    res = t[:].rearrange("p n i e -> p n (i e)")
+                else:
+                    eng.tensor_tensor(out=t[:, :, 0], in0=t[:, :, 0], in1=t[:, :, 1], op=ADD)
+                    res = t[:, :, 0].rearrange("p n i e -> p n (i e)")
+                nc.sync.dma_start(
+                    out=o_dst[nb][(i - 1) * P : (i + 1) * P, :].rearrange("(n p) c -> p n c", p=P), in_=res
                 )
+                return
+            if un in PADD:
+                bank = psa.tile([P, NB], F32, name="acc")
+                if is3(un):
+                    x0 = k1[un[0]][:, un[1], :].unsqueeze(2).to_broadcast([P, PAIRS, 2])
+                    x1 = xy[un][:]
+                else:
+                    x0, x1 = xy[un][:, 0], xy[un][:, 1]
+                view = bank[:].rearrange("p (i e) -> p i e", e=2)
+                nc.tensor.matmul(view, lhsT=ident[:], rhs=x0, start=True, stop=False)
+                nc.tensor.matmul(view, lhsT=negi[:] if is3(un) else ident[:], rhs=x1, start=False, stop=True)
+                o = vp.tile([P, NB], F32, name="vo")
+                nc.scalar.copy(out=o[:], in_=bank[:])
+                store(un, o[:])
+                return
+            parts = 1 if un in VADD else PIECES
+            if is3(un):
+                for q in range(parts):
+                    h = slice(q * PAIRS // parts, (q + 1) * PAIRS // parts)
+                    eng.tensor_tensor(
+                        out=xy[un][:, h, :],
+                        in0=k1[un[0]][:, un[1], h].unsqueeze(2).to_broadcast([P, PAIRS // parts, 2]),
+                        in1=xy[un][:, h, :],
+                        op=SUB,
+                    )
                 store(un, xy[un][:].rearrange("p i e -> p (i e)"))
                 return
             a = xy[un][:, 0]
             b = xy[un][:, 1]
-            eng.tensor_tensor(out=a, in0=a, in1=b, op=ADD)
+            for q in range(parts):
+                h = slice(q * PAIRS // parts, (q + 1) * PAIRS // parts)
+                eng.tensor_tensor(out=a[:, h], in0=a[:, h], in1=b[:, h], op=ADD)
             store(un, a.rearrange("p i e -> p (i e)"))
 
         def vcopy(un):
@@ -396,15 +512,10 @@ def tile_selfattn_pa_kernel(
 
         def unit(un):
             mm(un)
-            if un[1] in THREE:
-                mm_sum(un)
             if un[1] == 3:
                 vcopy(un)
                 return
-            if un[1] in THREE:
-                three_products(un)
-            else:
-                rope_products(un)
+            rope_products(un)
             flush()
             if un in VADD:
                 deferred.append((finish, un))
@@ -414,6 +525,12 @@ def tile_selfattn_pa_kernel(
         cast(0)
         cast(1)
         turn(0)
+        if WARM:
+            warm = psa.tile([P, NB], F32, name="acc")
+            for w in range(WARM):
+                nc.tensor.matmul(
+                    warm[:], lhsT=xbf[0][:, 0, 0:P], rhs=xbf[0][:, w % 2, 0:NB], start=True, stop=True
+                )
         for g in range(PASSES):
             for c0, c1, v in W0:
                 wcopy(0, g, c0, c1, v)
@@ -431,6 +548,15 @@ def tile_selfattn_pa_kernel(
             for g in range(PASSES):
                 for c1 in range(0, NB, GSTEP):
                     wcopy(nb, g, c1, c1 + GSTEP, "g")
+        ready = [0]
+        done = set()
+        for i in range(EARLY):
+            if is3((i, 0)):
+                qunit(i, [0])
+            else:
+                unit((i, 0))
+            done.add((i, 0))
+        flush()
         if 1 in SC_PAIRS:
             scale_on_scalar(1, 0)
             scale_on_scalar(1, 1)
@@ -439,8 +565,6 @@ def tile_selfattn_pa_kernel(
             scale(1, 1)
         quant(1)
 
-        ready = [0]
-        done = set()
         for i in range(NT):
             for nb in range(1, 4):
                 for g in range(PASSES):
@@ -473,9 +597,24 @@ def tile_selfattn_pa_kernel(
             order = [0, 1, 2, 3]
             if i == NT - 1:
                 order = [3, 0, 1, 2]
+            backlog = 0
             for j in range(i + 1):
+                if j < i and backlog >= CATCH and i < NT - 1:
+                    continue
+                nbs = []
+                for nb in THREE:
+                    if nb in ready and (j, nb) not in done and is3((j, nb)):
+                        nbs.append(nb)
                 for nb in order:
+                    if nb in nbs and nb == nbs[0]:
+                        qunit(j, nbs)
+                        for n in nbs:
+                            done.add((j, n))
+                        if j < i:
+                            backlog += 1
                     if nb in ready and (j, nb) not in done:
                         done.add((j, nb))
                         unit((j, nb))
+                        if j < i:
+                            backlog += 1
         flush()

from contextlib import ExitStack

import concourse.mybir as mybir
from concourse.masks import make_identity

F32 = mybir.dt.float32
BF16 = mybir.dt.bfloat16
U8 = mybir.dt.uint8
U32 = mybir.dt.uint32
FP8 = mybir.dt.float8_e4m3fn
FP8X4 = mybir.dt.float8_e4m3fn_x4
MULT = mybir.AluOpType.mult
ADD = mybir.AluOpType.add
SUB = mybir.AluOpType.subtract

P = 128
TOKENS = 2048
K = 1024
PASSES = 2
NT = TOKENS // P
NB = 512
PAIRS = NB // 2
FLOPS = 2 * TOKENS * K * 2048

SC_PAIRS = (4, 5, 6, 7)
VADD = ((5, 2), (6, 2), (7, 2), (8, 2), (9, 2), (10, 2), (11, 2), (12, 2), (13, 2), (14, 2), (15, 2), (15, 1))
THREE = (0,)
T3 = (16, 16)
PREP = {2: 0, 3: 3, 4: 6, 5: 8, 6: 10, 7: 12}
WPREP = {(1, 0): 2, (1, 1): 2, (2, 0): 3, (2, 1): 5, (3, 0): 5, (3, 1): 5}
TABENG = ("v", "v", "g", "g")
KTAB = 1
FAST = False
WARM = 0
EARLY = 0
CATCH = 2
JOIN = ()
PIECES = 1
PADD = ()
JLAST = 14
WPE = ()
VCAST = (0, 1)
WG = ()
GHEAD = ()
GSTEP = 128
LOADS = ("x0", "w0", "q0", "x1", "q1", "w1", "x2", "q2", "q3", "w2", "k", "x3", "w3", "x4", "x5", "x6", "x7")
QTAB = (0, 1, 2, 3)
WQ2 = False
QUADS = False
BUFR = 8
BUFQ = 8
BUFK = 4
BUFV = 4
W0 = ((0, 256, False), (256, 512, False))
COPY = mybir.ActivationFunctionType.Copy


def tile_selfattn_pa_kernel(
    tc, x_bytes, x_scale, Wq, Wk, Wv, cos_q, sin_q, cos_k, sin_k, out_0, out_1, out_2
):
    nc = tc.nc
    xf = x_bytes.flatten_outer_dims()
    oq = out_0.flatten_outer_dims()
    ok = out_1.flatten_outer_dims()
    ov = out_2.flatten_outer_dims()
    w_src = [Wq[:, 0:NB], Wq[:, NB : 2 * NB], Wk, Wv]
    o_dst = [oq[:, 0:NB], oq[:, NB : 2 * NB], ok, ov]

    with ExitStack() as ctx:
        keep = ctx.enter_context(tc.tile_pool(name="keep", bufs=1))
        xbfp = ctx.enter_context(tc.tile_pool(name="xbfp", bufs=2))
        xgp = ctx.enter_context(tc.tile_pool(name="xgp", bufs=2))
        xpp = ctx.enter_context(tc.tile_pool(name="xpp", bufs=2))
        wgp = ctx.enter_context(tc.tile_pool(name="wgp", bufs=2))
        rp = ctx.enter_context(tc.tile_pool(name="rp", bufs=BUFR))
        qp = ctx.enter_context(tc.tile_pool(name="qp", bufs=BUFQ))
        kp = ctx.enter_context(tc.tile_pool(name="kp", bufs=BUFK))
        jp = ctx.enter_context(tc.tile_pool(name="jp", bufs=3))
        vp = ctx.enter_context(tc.tile_pool(name="vp", bufs=BUFV))
        pst = ctx.enter_context(tc.psum_pool(name="pst", bufs=2))
        psa = ctx.enter_context(tc.psum_pool(name="psa", bufs=6))

        ident = keep.tile([P, P], F32, name="ident")
        make_identity(nc, ident[:])
        if len(PADD):
            negi = keep.tile([P, P], F32, name="negi")
            nc.gpsimd.tensor_scalar(out=negi[:], in0=ident[:], scalar1=-1.0, scalar2=0.0, op0=MULT, op1=ADD)
        plus = keep.tile([P, P], BF16, name="plus")
        if len(WPE):
            nc.vector.tensor_copy(out=plus[:], in_=ident[:])

        CS, SS = (2, 0) if len(THREE) == 2 else (0, 2)

        def is3(un):
            return un[1] in THREE and un[0] < T3[un[1]]

        sk = keep.tile([P, PASSES, 4], F32, name="sk")
        nc.sync.dma_start(
            out=sk[:], in_=x_scale.rearrange("a b k -> (a b k)").rearrange("(g p t) -> p g t", p=P, t=4)
        )
        xb = []
        wraw = []
        tq = []
        tk = keep.tile([P, 4, 4, PAIRS], BF16, name="tk")
        td = []
        for j in range(NT // 2):
            xb.append(keep.tile([P, 2, K], U8, name="xb%d" % j))
        for nb in range(4):
            wraw.append(keep.tile([P, PASSES, 4, NB], BF16, name="wraw%d" % nb))
        for tt in range(4):
            tq.append(keep.tile([P, 4, 2 * PAIRS], BF16, name="tq%d" % tt))
            td.append(keep.tile([P, 2, len(THREE) * PAIRS], F32, name="td%d" % tt))

        def load_x(j):
            nc.sync.dma_start(
                out=xb[j][:],
                in_=xf[2 * j * P : (2 * j + 2) * P, :].rearrange("(n p) k -> p n k", p=P),
            )

        def load_w(nb):
            for g in range(PASSES):
                nc.sync.dma_start(
                    out=wraw[nb][:, g],
                    in_=w_src[nb][g * 512 : (g + 1) * 512, :].rearrange("(p j) n -> p j n", j=4),
                )

        def load_tq(tt):
            nc.sync.dma_start(out=tq[tt][:, SS, :], in_=sin_q[tt * P : (tt + 1) * P, :])
            nc.sync.dma_start(out=tq[tt][:, CS, :], in_=cos_q[tt * P : (tt + 1) * P, :])

        def load_tk(tt):
            nc.sync.dma_start(out=tk[:, 2, tt, :], in_=sin_k[tt * P : (tt + 1) * P, :])
            nc.sync.dma_start(out=tk[:, 0, tt, :], in_=cos_k[tt * P : (tt + 1) * P, :])

        for what in LOADS:
            if what == "k":
                for tt in range(4):
                    load_tk(tt)
            elif what[0] == "x":
                load_x(int(what[1]))
            elif what[0] == "w":
                load_w(int(what[1]))
            else:
                load_tq(int(what[1]))

        def sumdiff(tt, eng):
            c = slice(0, len(THREE) * PAIRS)
            for e, op in ((0, SUB), (1, ADD)):
                eng.tensor_tensor(out=td[tt][:, e, :], in0=tq[tt][:, CS, c], in1=tq[tt][:, SS, c], op=op)

        def qtables(tt):
            eng = nc.gpsimd if TABENG[tt] == "g" else nc.vector
            if len(THREE):
                sumdiff(tt, eng)
            b0, b1 = 2, 0
            for nb in range(2):
                if nb not in THREE or T3[nb] < NT:
                    b0, b1 = min(b0, nb), nb + 1
            if b0 >= b1:
                return
            c = slice(b0 * PAIRS, b1 * PAIRS)
            if TABENG[tt] == "g":
                eng.tensor_scalar(
                    out=tq[tt][:, CS + 1, c], in0=tq[tt][:, SS, c], scalar1=-1.0, scalar2=0.0, op0=MULT, op1=ADD
                )
                eng.tensor_scalar(
                    out=tq[tt][:, SS + 1, c], in0=tq[tt][:, CS, c], scalar1=1.0, scalar2=0.0, op0=MULT, op1=ADD
                )
            else:
                eng.tensor_scalar(out=tq[tt][:, CS + 1, c], in0=tq[tt][:, SS, c], scalar1=-1.0, scalar2=None, op0=MULT)
                eng.tensor_copy(out=tq[tt][:, SS + 1, c], in_=tq[tt][:, CS, c])

        def ktables():
            nc.vector.tensor_scalar(out=tk[:, 1], in0=tk[:, 2], scalar1=-1.0, scalar2=None, op0=MULT)
            nc.vector.tensor_copy(out=tk[:, 3], in_=tk[:, 0])

        xbf = {}
        xt = {}
        xg = {}
        xc = {}
        xs = {}
        xpl = {}

        def quad(j):
            return j if j < 2 or not QUADS else 1 + j // 2

        def pairs_of(q):
            return (q,) if q < 2 or not QUADS else (2 * q - 2, 2 * q - 1)


        def cast(i):
            j, n = divmod(i, 2)
            if n == 0:
                xbf[j] = xbfp.tile([P, 2, K], BF16, name="xbf")
            if i in VCAST:
                nc.vector.tensor_copy(out=xbf[j][:, n, :], in_=xb[j][:, n, :].bitcast(FP8))
            else:
                nc.scalar.copy(out=xbf[j][:, n, :], in_=xb[j][:, n, :].bitcast(FP8))

        def turn(j):
            for g in range(PASSES):
                xt[(j, g)] = pst.tile([P, 2, 2, P], F32, name="xt")
                for n in range(2):
                    words = xbf[j][:, n, :].bitcast(F32)
                    for u in range(2):
                        nc.tensor.transpose(
                            xt[(j, g)][:, u, n, :], words[:, 256 * g + u : 256 * (g + 1) : 2], ident[:]
                        )

        def halfwords(j, g):
            return xt[(j, g)][:].rearrange("p u n r -> p u (n r)").bitcast(BF16)

        def staging(j):
            q = quad(j)
            if q not in xg:
                n = len(pairs_of(q))
                xg[q] = xgp.tile([P, n, PASSES, 2 * P, 4], BF16, name="xg%d" % n, align_bytes=64)
            return xg[q][:, j - pairs_of(q)[0]]

        def scale(j, g):
            nc.vector.tensor_tensor(
                out=staging(j)[:, g].rearrange("p m (u e) -> p m u e", u=2),
                in0=halfwords(j, g).rearrange("p u (m e) -> p m u e", e=2),
                in1=sk[:, g, :]
                .rearrange("p (u e) -> p u e", u=2)
                .unsqueeze(1)
                .to_broadcast([P, 2 * P, 2, 2]),
                op=MULT,
            )

        def scale_on_scalar(j, g):
            if g == 0:
                xpl[j] = xpp.tile([P, PASSES, 4, 2 * P], BF16, name="xpl")
            for u in range(2):
                halves = halfwords(j, g)[:, u, :].rearrange("p (m e) -> p m e", e=2)
                for e in range(2):
                    t = 2 * u + e
                    nc.scalar.activation(
                        out=xpl[j][:, g, t, :],
                        in_=halves[:, :, e],
                        func=COPY,
                        scale=sk[:, g, t : t + 1],
                    )
            if g == PASSES - 1:
                if FAST:
                    for q in range(PASSES):
                        nc.scalar.copy(
                            out=staging(j)[:, q].rearrange("p (c i) t -> p c t i", i=4),
                            in_=xpl[j][:, q].rearrange("p t (c i) -> p c t i", i=4),
                        )
                else:
                    nc.scalar.copy(out=staging(j), in_=xpl[j][:].rearrange("p g t m -> p g m t"))

        def quant(q):
            n = len(pairs_of(q))
            codes = keep.tile([P, n, PASSES, 2 * P], U32, name="xc%d" % q, align_bytes=64)
            scales = keep.tile([P, n, PASSES, 2 * P], U8, name="xs%d" % q, align_bytes=64)
            nc.vector.quantize_mx(
                out=codes[:].rearrange("p n g m -> p (n g m)").bitcast(FP8X4),
                scales=scales[:].rearrange("p n g m -> p (n g m)"),
                in_=xg[q][:].rearrange("p n g m t -> p (n g m t)"),
            )
            for j in pairs_of(q):
                xc[j] = codes[:, j - pairs_of(q)[0]]
                xs[j] = scales[:, j - pairs_of(q)[0]]

        wg = {}
        wc = []
        ws = []
        for nb in range(4):
            wc.append(keep.tile([P, PASSES, NB], U32, name="wc%d" % nb, align_bytes=64))
            ws.append(keep.tile([P, PASSES, NB], U8, name="ws%d" % nb, align_bytes=64))

        def winter(nb, g, c0, c1):
            if nb not in wg:
                wg[nb] = wgp.tile([P, PASSES, NB, 4], BF16, name="wg", align_bytes=64)
            bank = psa.tile([P, NB // 2, 4], BF16, name="acc")
            for j in range(4):
                nc.tensor.matmul(
                    bank[:, :, j], lhsT=plus[:], rhs=wraw[nb][:, g, j, c0:c1], start=True, stop=True
                )
            nc.scalar.copy(out=wg[nb][:, g, c0:c1, :], in_=bank[:])

        def wcopy(nb, g, c0, c1, on_vector):
            if nb not in wg:
                wg[nb] = wgp.tile([P, PASSES, NB, 4], BF16, name="wg", align_bytes=64)
            dst = wg[nb][:, g, c0:c1, :]
            if nb in THREE:
                e, i0 = divmod(c0, PAIRS)
                first = 2 * i0 + 1 - e
                src = wraw[nb][:, g, :, first : first + 2 * (c1 - c0) - 1 : 2].rearrange("p j n -> p n j")
            else:
                src = wraw[nb][:, g, :, c0:c1].rearrange("p j n -> p n j")
            if FAST:
                dst = dst.rearrange("p (c i) t -> p c t i", i=4)
                src = src.rearrange("p (c i) t -> p c t i", i=4)
            if on_vector == "g":
                nc.gpsimd.tensor_scalar(out=dst, in0=src, scalar1=1.0, scalar2=0.0, op0=MULT, op1=ADD)
            elif on_vector:
                nc.vector.tensor_copy(out=dst, in_=src)
            else:
                nc.scalar.copy(out=dst, in_=src)

        def wquant(nb, g0, g1):
            nc.vector.quantize_mx(
                out=wc[nb][:, g0:g1, :].rearrange("p g n -> p (g n)").bitcast(FP8X4),
                scales=ws[nb][:, g0:g1, :].rearrange("p g n -> p (g n)"),
                in_=wg[nb][:, g0:g1].rearrange("p g n j -> p (g n j)"),
            )

        acc = {}
        xy = {}

        def mm(un):
            i, nb = un
            acc[un] = psa.tile([P, NB], F32, name="acc")
            for g in range(PASSES):
                nc.tensor.matmul_mx(
                    out=acc[un][:],
                    lhsT=xc[i // 2][:, g, (i % 2) * P : (i % 2 + 1) * P].bitcast(FP8X4),
                    lhsT_scale=xs[i // 2][:, g, (i % 2) * P : (i % 2 + 1) * P],
                    rhs=wc[nb][:, g, :].bitcast(FP8X4),
                    rhs_scale=ws[nb][:, g, :],
                    start=(g == 0),
                    stop=(g == PASSES - 1),
                )

        ysum = {}
        k1 = {}

        def mm_sum(un):
            i, nb = un
            if ysum.get(i) is None:
                ysum[i] = psa.tile([P, 2, PAIRS], F32, name="acc")
            for g in range(PASSES):
                for e in range(2):
                    cols = slice(e * PAIRS, (e + 1) * PAIRS)
                    nc.tensor.matmul_mx(
                        out=ysum[i][:, nb, :],
                        lhsT=xc[i // 2][:, g, (i % 2) * P : (i % 2 + 1) * P].bitcast(FP8X4),
                        lhsT_scale=xs[i // 2][:, g, (i % 2) * P : (i % 2 + 1) * P],
                        rhs=wc[nb][:, g, cols].bitcast(FP8X4),
                        rhs_scale=ws[nb][:, g, cols],
                        start=(g == 0 and e == 0),
                        stop=(g == PASSES - 1 and e == 1),
                    )

        def sum_product(i, nbs):
            n0, n1 = nbs[0], nbs[-1] + 1
            if len(JOIN) and joined((i, nbs[0])):
                if i % 2 == 0:
                    k1j[i // 2] = kp.tile([P, 2, 2, PAIRS], F32, name="k1j")
                k1[i] = k1j[i // 2][:, i % 2]
            else:
                k1[i] = kp.tile([P, 2, PAIRS], F32, name="k1")
            nc.vector.tensor_tensor(
                out=k1[i][:, n0:n1, :],
                in0=ysum[i][:, n0:n1, :],
                in1=tq[i % 4][:, CS, n0 * PAIRS : n1 * PAIRS].rearrange("p (b i) -> p b i", i=PAIRS),
                op=MULT,
            )

        def three_products(un):
            i, nb = un
            if joined(un):
                if i % 2 == 0:
                    joint[(i // 2, nb)] = jp.tile([P, 2, PAIRS, 2], F32, name="jq%d" % nb)
                dst = joint[(i // 2, nb)][:, i % 2]
            else:
                xy[un] = qp.tile([P, PAIRS, 2], F32, name="qxy")
                dst = xy[un][:]
            nc.vector.tensor_tensor(
                out=dst,
                in0=acc[un][:].rearrange("p (e i) -> p i e", e=2),
                in1=td[i % 4][:, :, nb * PAIRS : (nb + 1) * PAIRS].rearrange("p e i -> p i e"),
                op=MULT,
            )

        def qunit(i, nbs):
            for nb in nbs:
                mm((i, nb))
                mm_sum((i, nb))
            sum_product(i, nbs)
            for nb in nbs:
                un = (i, nb)
                three_products(un)
                flush()
                if un in VADD:
                    deferred.append((finish, un))
                else:
                    finish(un)
            ysum[i] = None

        def table(un):
            i, nb = un
            if nb == 2:
                return tk[:, :, i % 4, :]
            return tq[i % 4][:, :, nb * PAIRS : (nb + 1) * PAIRS]

        joint = {}
        k1j = {}

        def joined(un):
            return un[1] in JOIN and un[0] < JLAST and un not in VADD and (un[0] ^ 1, un[1]) not in VADD

        def rope_products(un):
            if joined(un):
                i, nb = un
                if i % 2 == 0:
                    joint[(i // 2, nb)] = jp.tile([P, 2, 2, PAIRS, 2], F32, name="jr%d" % nb)
                dst = joint[(i // 2, nb)][:, i % 2]
            else:
                xy[un] = rp.tile([P, 2, PAIRS, 2], F32, name="rxy")
                dst = xy[un][:]
            nc.vector.tensor_tensor(
                out=dst,
                in0=acc[un][:]
                .rearrange("p (e i) -> p e i" if un[1] in THREE else "p (i e) -> p e i", e=2)
                .unsqueeze(3)
                .to_broadcast([P, 2, PAIRS, 2]),
                in1=table(un).rearrange("p (e h) i -> p e i h", e=2),
                op=MULT,
            )

        def store(un, src):
            i, nb = un
            nc.sync.dma_start(out=o_dst[nb][i * P : (i + 1) * P, :], in_=src)

        def finish(un):
            eng = nc.gpsimd
            if un in VADD:
                eng = nc.vector
            if joined(un):
                i, nb = un
                if i % 2 == 0:
                    return
                t = joint[(i // 2, nb)]
                if is3(un):
                    eng.tensor_tensor(
                        out=t[:],
                        in0=k1j[i // 2][:, :, nb, :].unsqueeze(3).to_broadcast([P, 2, PAIRS, 2]),
                        in1=t[:],
                        op=SUB,
                    )
                    res = t[:].rearrange("p n i e -> p n (i e)")
                else:
                    eng.tensor_tensor(out=t[:, :, 0], in0=t[:, :, 0], in1=t[:, :, 1], op=ADD)
                    res = t[:, :, 0].rearrange("p n i e -> p n (i e)")
                nc.sync.dma_start(
                    out=o_dst[nb][(i - 1) * P : (i + 1) * P, :].rearrange("(n p) c -> p n c", p=P), in_=res
                )
                return
            if un in PADD:
                bank = psa.tile([P, NB], F32, name="acc")
                if is3(un):
                    x0 = k1[un[0]][:, un[1], :].unsqueeze(2).to_broadcast([P, PAIRS, 2])
                    x1 = xy[un][:]
                else:
                    x0, x1 = xy[un][:, 0], xy[un][:, 1]
                view = bank[:].rearrange("p (i e) -> p i e", e=2)
                nc.tensor.matmul(view, lhsT=ident[:], rhs=x0, start=True, stop=False)
                nc.tensor.matmul(view, lhsT=negi[:] if is3(un) else ident[:], rhs=x1, start=False, stop=True)
                o = vp.tile([P, NB], F32, name="vo")
                nc.scalar.copy(out=o[:], in_=bank[:])
                store(un, o[:])
                return
            parts = 1 if un in VADD else PIECES
            if is3(un):
                for q in range(parts):
                    h = slice(q * PAIRS // parts, (q + 1) * PAIRS // parts)
                    eng.tensor_tensor(
                        out=xy[un][:, h, :],
                        in0=k1[un[0]][:, un[1], h].unsqueeze(2).to_broadcast([P, PAIRS // parts, 2]),
                        in1=xy[un][:, h, :],
                        op=SUB,
                    )
                store(un, xy[un][:].rearrange("p i e -> p (i e)"))
                return
            a = xy[un][:, 0]
            b = xy[un][:, 1]
            for q in range(parts):
                h = slice(q * PAIRS // parts, (q + 1) * PAIRS // parts)
                eng.tensor_tensor(out=a[:, h], in0=a[:, h], in1=b[:, h], op=ADD)
            store(un, a.rearrange("p i e -> p (i e)"))

        def vcopy(un):
            o = vp.tile([P, NB], F32, name="vo")
            nc.scalar.copy(out=o[:], in_=acc[un][:])
            store(un, o[:])

        deferred = []

        def flush():
            for fn, arg in deferred:
                fn(arg)
            deferred.clear()

        def xprep(j, g):
            if j >= NT // 2:
                return
            if g == 0:
                cast(2 * j)
                cast(2 * j + 1)
                turn(j)
            if j in SC_PAIRS:
                scale_on_scalar(j, g)
            else:
                scale(j, g)
            if g == PASSES - 1:
                if j == pairs_of(quad(j))[-1]:
                    deferred.append((quant, quad(j)))

        def unit(un):
            mm(un)
            if un[1] == 3:
                vcopy(un)
                return
            rope_products(un)
            flush()
            if un in VADD:
                deferred.append((finish, un))
            else:
                finish(un)

        cast(0)
        cast(1)
        turn(0)
        if WARM:
            warm = psa.tile([P, NB], F32, name="acc")
            for w in range(WARM):
                nc.tensor.matmul(
                    warm[:], lhsT=xbf[0][:, 0, 0:P], rhs=xbf[0][:, w % 2, 0:NB], start=True, stop=True
                )
        for g in range(PASSES):
            for c0, c1, v in W0:
                wcopy(0, g, c0, c1, v)
            scale(0, g)
        wquant(0, 0, 1)
        quant(0)
        wquant(0, 1, 2)
        cast(2)
        cast(3)
        turn(1)
        for tt in range(4):
            if QTAB[tt] < 0:
                qtables(tt)
        for nb in GHEAD:
            for g in range(PASSES):
                for c1 in range(0, NB, GSTEP):
                    wcopy(nb, g, c1, c1 + GSTEP, "g")
        ready = [0]
        done = set()
        for i in range(EARLY):
            if is3((i, 0)):
                qunit(i, [0])
            else:
                unit((i, 0))
            done.add((i, 0))
        flush()
        if 1 in SC_PAIRS:
            scale_on_scalar(1, 0)
            scale_on_scalar(1, 1)
        else:
            scale(1, 0)
            scale(1, 1)
        quant(1)

        for i in range(NT):
            for nb in range(1, 4):
                for g in range(PASSES):
                    if WPREP[nb, g] == i:
                        for c0 in (0, NB // 2):
                            if nb in GHEAD:
                                continue
                            if (nb, g, c0) in WG:
                                for c1 in range(c0, c0 + 256, 128):
                                    wcopy(nb, g, c1, c1 + 128, "g")
                            elif nb in WPE:
                                winter(nb, g, c0, c0 + NB // 2)
                            else:
                                wcopy(nb, g, c0, c0 + NB // 2, False)
                        if not WQ2:
                            wquant(nb, g, g + 1)
                        elif g == PASSES - 1:
                            wquant(nb, 0, PASSES)
                        if g == PASSES - 1:
                            ready.append(nb)
            for tt in range(4):
                if QTAB[tt] == i:
                    qtables(tt)
            if i == KTAB:
                ktables()
            for j in range(2, NT // 2):
                for g in range(PASSES):
                    if PREP[j] + g == i:
                        xprep(j, g)
            order = [0, 1, 2, 3]
            if i == NT - 1:
                order = [3, 0, 1, 2]
            backlog = 0
            for j in range(i + 1):
                if j < i and backlog >= CATCH and i < NT - 1:
                    continue
                nbs = []
                for nb in THREE:
                    if nb in ready and (j, nb) not in done and is3((j, nb)):
                        nbs.append(nb)
                for nb in order:
                    if nb in nbs and nb == nbs[0]:
                        qunit(j, nbs)
                        for n in nbs:
                            done.add((j, n))
                        if j < i:
                            backlog += 1
                    if nb in ready and (j, nb) not in done:
                        done.add((j, nb))
                        unit((j, nb))
                        if j < i:
                            backlog += 1
        flush()
